import numpy as np
import ml_dtypes


def mxq(x, axis, fmt="e4m3"):
    dtype, down = {"e4m3": (ml_dtypes.float8_e4m3fn, 7), "e5m2": (ml_dtypes.float8_e5m2, 14)}[fmt]
    v = np.moveaxis(np.asarray(x, np.float32).astype(ml_dtypes.bfloat16).astype(np.float64), axis, -1)
    blocks = v.reshape(v.shape[:-1] + (-1, 32))
    amax = np.abs(blocks).max(-1, keepdims=True)
    byte = np.maximum(np.where(amax > 0, np.frexp(amax)[1] - 1 + 127, 0) - down, 1)
    scale = np.exp2(byte - 127.0)
    codes = (blocks / scale).astype(np.float32).astype(dtype).astype(np.float64)
    return np.moveaxis((codes * scale).reshape(v.shape), -1, axis)


WIDE = False


def mx_kscale(k):
    if not WIDE:
        return np.ones(k)
    levels = np.array([10, -10, 5, -5, 0])
    a = np.random.permutation(np.resize(levels, k // 512 * 4)).reshape(k // 512, 4)
    idx = np.arange(k)
    return np.exp2(a[idx // 512, idx % 128 // 32])


BF16 = ml_dtypes.bfloat16


def bf(x):
    return np.asarray(x, np.float32).astype(BF16)


def f64(x):
    return np.asarray(x).astype(np.float64)


T, B, D, U, V, E = 4, 8192, 1024, 16, 512, 8
G = 2 * E
GS = (T + 1) * E


def softmax(v):
    e = np.exp(v - v.max(-1, keepdims=True))
    return e / e.sum(-1, keepdims=True)


def setup_inputs():
    rn = np.random.standard_normal
    s = mx_kscale(D)
    return {
        "x": bf(rn((B, D)) * s),
        "ews0": bf(rn((D, U, E)) / np.sqrt(D) / s[:, None, None]),
        "ebs0": bf(rn((U, E)) * 0.5),
        "ew0": bf(rn((T, D, U, E)) / np.sqrt(D) / s[None, :, None, None]),
        "eb0": bf(rn((T, U, E)) * 0.5),
        "gate_pre0": bf(rn((T, B, G))),
        "gb0": bf(rn((T, G)) * 0.5),
        "sgate_pre": bf(rn((B, GS))),
        "gbs": bf(rn((GS,)) * 0.5),
    }


def reference(x, ews0, ebs0, ew0, eb0, gate_pre0, gb0, sgate_pre, gbs):
    xq = mxq(f64(x), 1, "e4m3")
    es = np.maximum((xq @ mxq(f64(ews0).reshape(D, U * E), 0, "e4m3")).reshape(B, U, E) + f64(ebs0), 0.0)
    et = np.maximum((xq @ mxq(f64(ew0).reshape(T, D, U * E), 1, "e4m3")).reshape(T, B, U, E) + f64(eb0)[:, None], 0.0)
    g = softmax(f64(gate_pre0) + f64(gb0)[:, None])
    comb = np.concatenate([et, np.broadcast_to(es, et.shape)], axis=-1)
    task_out = (comb * g[:, :, None, :]).sum(-1)
    gs = softmax(f64(sgate_pre) + f64(gbs))
    all_exp = np.concatenate([np.moveaxis(et, 0, 2).reshape(B, U, T * E), es], axis=-1)
    share_out = (all_exp * gs[:, None, :]).sum(-1)
    return task_out, share_out

@@ -1,0 +1,359 @@
+from contextlib import ExitStack
+
+import concourse.mybir as mybir
+from concourse.masks import make_identity
+
+F32 = mybir.dt.float32
+BF16 = mybir.dt.bfloat16
+U32 = mybir.dt.uint32
+U8 = mybir.dt.uint8
+FP8X4 = mybir.dt.float8_e4m3fn_x4
+ALU = mybir.AluOpType
+ACT = mybir.ActivationFunctionType
+AXIS_X = mybir.AxisListType.X
+
+P = 128
+T, B, D, U, E = 4, 8192, 1024, 16, 8
+SOURCES = T + 1
+SHARED = T
+UE = U * E
+G_TASK = 2 * E
+G_SHARE = SOURCES * E
+PACK = 4
+K_PASS = P * PACK
+PASSES = D // K_PASS
+ROW_TILES = B // P
+ROUND = 4
+ROUNDS = ROW_TILES // ROUND
+COLS = ROUND * P
+GATE_CHUNK = 16
+STORE_ROUNDS = 4
+SLOTS_USED = SOURCES * U
+
+FLOPS = 2 * B * D * SOURCES * UE
+
+
+def tile_plelayer_pa_t_kernel(
+    tc, x, ews0, ebs0, ew0, eb0, gate_pre0, gb0, sgate_pre, gbs, out_0, out_1
+):
+    nc = tc.nc
+    with ExitStack() as ctx:
+        keep = ctx.enter_context(tc.tile_pool(name="keep", bufs=1))
+        gate_tmp = ctx.enter_context(tc.tile_pool(name="gate_tmp", bufs=2))
+        x_pool = ctx.enter_context(tc.tile_pool(name="x_pool", bufs=3))
+        quant = ctx.enter_context(tc.tile_pool(name="quant", bufs=2))
+        work = ctx.enter_context(tc.tile_pool(name="work", bufs=2))
+        prod = ctx.enter_context(tc.tile_pool(name="prod", bufs=6))
+        ps_xt = ctx.enter_context(tc.psum_pool(name="ps_xt", bufs=2))
+        ps_y = ctx.enter_context(tc.psum_pool(name="ps_y", bufs=2))
+        ps_ra = ctx.enter_context(tc.psum_pool(name="ps_ra", bufs=2))
+        ps_misc = ctx.enter_context(tc.psum_pool(name="ps_misc", bufs=2))
+
+        x_rows = x.rearrange("(p n) k -> p n k", n=ROW_TILES)
+        out_task_rows = out_0.rearrange("t (p n) u -> p t n u", n=ROW_TILES)
+        out_share_rows = out_1.rearrange("(p n) u -> p n u", n=ROW_TILES)
+
+        ident = keep.tile([P, P], F32)
+        make_identity(nc, ident[:])
+
+        w_raw = keep.tile([P, SOURCES, 2 * PASSES, 2, UE], BF16)
+        for t in range(T):
+            nc.sync.dma_start(
+                out=w_raw[:, t],
+                in_=ew0[t].rearrange("(a q c) u e -> q a c (u e)", a=2 * PASSES, c=2),
+            )
+        nc.sync.dma_start(
+            out=w_raw[:, SHARED],
+            in_=ews0.rearrange("(a q c) u e -> q a c (u e)", a=2 * PASSES, c=2),
+        )
+
+        def load_x(r):
+            x_sb = x_pool.tile([P, ROUND, D], BF16)
+            nc.sync.dma_start(out=x_sb[:], in_=x_rows[:, r * ROUND : (r + 1) * ROUND, :])
+            return x_sb
+
+        x_first = load_x(0)
+
+        w_grouped = keep.tile([P, PASSES, SOURCES, UE, PACK], BF16, align_bytes=64)
+        w_codes = keep.tile([P, PASSES, SOURCES * UE], U32, align_bytes=64)
+        w_scales = keep.tile([P, PASSES, SOURCES * UE], U8, align_bytes=64)
+        for g in range(PASSES):
+            for t in range(T):
+                nc.vector.tensor_copy(
+                    out=w_grouped[:, g, t].rearrange("q (e u) (a c) -> q e u a c", e=E, a=2),
+                    in_=w_raw[:, t, 2 * g : 2 * g + 2].rearrange("q a c (u e) -> q e u a c", u=U),
+                )
+            nc.vector.tensor_copy(
+                out=w_grouped[:, g, SHARED].rearrange("q k (a c) -> q k a c", a=2),
+                in_=w_raw[:, SHARED, 2 * g : 2 * g + 2].rearrange("q a c k -> q k a c"),
+            )
+        for g in range(PASSES):
+            nc.vector.quantize_mx(
+                out=w_codes[:, g, 0 : T * UE].bitcast(FP8X4),
+                scales=w_scales[:, g, 0 : T * UE],
+                in_=w_grouped[:, g, 0:T].rearrange("q s k j -> q (s k j)"),
+            )
+            nc.vector.quantize_mx(
+                out=w_codes[:, g, T * UE : SOURCES * UE].bitcast(FP8X4),
+                scales=w_scales[:, g, T * UE : SOURCES * UE],
+                in_=w_grouped[:, g, SHARED].rearrange("q k j -> q (k j)"),
+            )
+
+        SHARED_ROW = 32
+        bias_rows = keep.tile([P, UE], BF16)
+        nc.scalar.dma_start(out=bias_rows[0:T, :], in_=eb0.rearrange("t u e -> t (u e)"))
+        nc.scalar.dma_start(
+            out=bias_rows[SHARED_ROW : SHARED_ROW + 1, :],
+            in_=ebs0.rearrange("(o u) e -> o (u e)", o=1),
+        )
+        bias_square = keep.tile([P, P], F32)
+        nc.vector.memset(bias_square[:], 0.0)
+        nc.vector.tensor_copy(
+            out=bias_square[0:T, :].rearrange("t (e u) -> t e u", e=E),
+            in_=bias_rows[0:T, :].rearrange("t (u e) -> t e u", e=E),
+        )
+        nc.vector.tensor_copy(
+            out=bias_square[SHARED_ROW : SHARED_ROW + 1, :],
+            in_=bias_rows[SHARED_ROW : SHARED_ROW + 1, :],
+        )
+        bias_ps = ps_misc.tile([P, P], F32, tag="misc")
+        nc.tensor.transpose(out=bias_ps[:], in_=bias_square[:], identity=ident[:])
+        bias_cols = keep.tile([P, P], F32)
+        nc.vector.tensor_copy(out=bias_cols[:], in_=bias_ps[:])
+        bias_col_of = [t for t in range(T)] + [SHARED_ROW]
+
+        gate_bias_task = keep.tile([P, T, G_TASK], BF16)
+        nc.scalar.dma_start(
+            out=gate_bias_task[:].rearrange("p t k -> p (t k)"),
+            in_=gb0.rearrange("t k -> (t k)").partition_broadcast(P),
+        )
+        gate_bias_share = keep.tile([P, G_SHARE], BF16)
+        nc.scalar.dma_start(out=gate_bias_share[:], in_=gbs.partition_broadcast(P))
+        pre_task = keep.tile([P, T, ROW_TILES, G_TASK], BF16)
+        for t in range(T):
+            nc.scalar.dma_start(
+                out=pre_task[:, t], in_=gate_pre0[t].rearrange("(p n) k -> p n k", n=ROW_TILES)
+            )
+        pre_share = keep.tile([P, ROW_TILES, G_SHARE], BF16)
+        nc.scalar.dma_start(
+            out=pre_share[:], in_=sgate_pre.rearrange("(p n) k -> p n k", n=ROW_TILES)
+        )
+
+        gates_own = keep.tile([P, ROW_TILES, 2, E, T], F32)
+        gates_shared = keep.tile([P, ROW_TILES, SOURCES, E], F32)
+
+        def softmax_in_place(logits, groups_shape, width):
+            full_shape = [P] + groups_shape + [width]
+            last = len(groups_shape) + 1
+            top = gate_tmp.tile([P] + groups_shape, F32, name="top", tag="top%d" % width)
+            nc.vector.tensor_reduce(out=top[:], in_=logits[:], axis=AXIS_X, op=ALU.max)
+            nc.gpsimd.tensor_tensor(
+                out=logits[:],
+                in0=logits[:],
+                in1=top[:].unsqueeze(last).to_broadcast(full_shape),
+                op=ALU.subtract,
+            )
+            nc.scalar.activation(out=logits[:], in_=logits[:], func=ACT.Exp)
+            total = gate_tmp.tile([P] + groups_shape, F32, name="total", tag="total%d" % width)
+            nc.vector.tensor_reduce(out=total[:], in_=logits[:], axis=AXIS_X, op=ALU.add)
+            inverse = gate_tmp.tile([P] + groups_shape, F32, name="inverse", tag="inv%d" % width)
+            nc.vector.reciprocal(out=inverse[:], in_=total[:])
+            return inverse
+
+        def make_gates(chunk):
+            rows = slice(chunk * GATE_CHUNK, (chunk + 1) * GATE_CHUNK)
+            C = GATE_CHUNK
+            task = gate_tmp.tile([P, T, C, G_TASK], F32)
+            nc.gpsimd.tensor_tensor(
+                out=task[:],
+                in0=pre_task[:, :, rows, :],
+                in1=gate_bias_task[:].unsqueeze(2).to_broadcast([P, T, C, G_TASK]),
+                op=ALU.add,
+            )
+            share = gate_tmp.tile([P, C, G_SHARE], F32)
+            nc.gpsimd.tensor_tensor(
+                out=share[:],
+                in0=pre_share[:, rows, :],
+                in1=gate_bias_share[:].unsqueeze(1).to_broadcast([P, C, G_SHARE]),
+                op=ALU.add,
+            )
+            task_inv = softmax_in_place(task, [T, C], G_TASK)
+            share_inv = softmax_in_place(share, [C], G_SHARE)
+            task_inv_nt = task_inv[:].rearrange("p t n -> p n t")
+            nc.gpsimd.tensor_tensor(
+                out=gates_own[:, rows, 0, :, :],
+                in0=task[:, :, :, 0:E].rearrange("p t n e -> p n e t"),
+                in1=task_inv_nt.unsqueeze(2).to_broadcast([P, C, E, T]),
+                op=ALU.mult,
+            )
+            nc.gpsimd.tensor_tensor(
+                out=gates_shared[:, rows, 0:T, :],
+                in0=task[:, :, :, E:G_TASK].rearrange("p t n e -> p n t e"),
+                in1=task_inv_nt.unsqueeze(3).to_broadcast([P, C, T, E]),
+                op=ALU.mult,
+            )
+            nc.gpsimd.tensor_tensor(
+                out=gates_own[:, rows, 1, :, :],
+                in0=share[:, :, 0 : T * E].rearrange("p n (t e) -> p n e t", t=T),
+                in1=share_inv[:].unsqueeze(2).unsqueeze(3).to_broadcast([P, C, E, T]),
+                op=ALU.mult,
+            )
+            nc.gpsimd.tensor_tensor(
+                out=gates_shared[:, rows, SHARED, :],
+                in0=share[:, :, T * E : G_SHARE],
+                in1=share_inv[:].unsqueeze(2).to_broadcast([P, C, E]),
+                op=ALU.mult,
+            )
+
+        shared_sum_a = keep.tile([P, ROUND, P], F32)
+        shared_sum_b = keep.tile([P, ROUND, P], F32)
+        shared_sums = [shared_sum_a, shared_sum_b]
+        for shared_sum in shared_sums:
+            nc.vector.memset(shared_sum[:], 0.0)
+
+        x_next = x_first
+        for r in range(ROUNDS):
+            if r % (GATE_CHUNK // ROUND) == 0:
+                make_gates(r // (GATE_CHUNK // ROUND))
+            x_sb = x_next
+            if r + 1 < ROUNDS:
+                x_next = load_x(r + 1)
+
+            x_words = x_sb[:].bitcast(F32)
+            x_grouped = quant.tile([P, PASSES, ROUND, P, PACK], BF16, align_bytes=64)
+            x_grouped_words = x_grouped[:].bitcast(F32)
+            for i in range(ROUND):
+                xt_ps = ps_xt.tile([P, 2 * PASSES, P], F32)
+                for a in range(2 * PASSES):
+                    nc.tensor.transpose(
+                        out=xt_ps[:, a, :],
+                        in_=x_words[:, i, a * P : (a + 1) * P],
+                        identity=ident[:],
+                    )
+                nc.scalar.copy(
+                    out=x_grouped_words[:, :, i, :, :],
+                    in_=xt_ps[:].rearrange("q (g a) b -> q g b a", g=PASSES),
+                )
+            x_codes = quant.tile([P, PASSES, COLS], U32, align_bytes=64)
+            x_scales = quant.tile([P, PASSES, COLS], U8, align_bytes=64)
+            for g in range(PASSES):
+                nc.vector.quantize_mx(
+                    out=x_codes[:, g, :].bitcast(FP8X4),
+                    scales=x_scales[:, g, :],
+                    in_=x_grouped[:, g].rearrange("q i b j -> q (i b j)"),
+                )
+
+            experts = work.tile([P, SOURCES, COLS], F32)
+            for s in range(SOURCES):
+                y_ps = ps_y.tile([P, COLS], F32)
+                for g in range(PASSES):
+                    nc.tensor.matmul_mx(
+                        out=y_ps[:],
+                        lhsT=w_codes[:, g, s * UE : (s + 1) * UE].bitcast(FP8X4),
+                        lhsT_scale=w_scales[:, g, s * UE : (s + 1) * UE],
+                        rhs=x_codes[:, g, :].bitcast(FP8X4),
+                        rhs_scale=x_scales[:, g, :],
+                        start=(g == 0),
+                        stop=(g == PASSES - 1),
+                    )
+                nc.scalar.activation(
+                    out=experts[:, s, :],
+                    in_=y_ps[:],
+                    func=ACT.Relu,
+                    bias=bias_cols[:, bias_col_of[s] : bias_col_of[s] + 1],
+                    scale=1.0,
+                )
+
+            shared_ps = ps_misc.tile([P, ROUND, UE], F32, tag="misc")
+            for i in range(ROUND):
+                nc.tensor.transpose(
+                    out=shared_ps[:, i, :],
+                    in_=experts[:, SHARED, i * P : (i + 1) * P],
+                    identity=ident[:],
+                )
+            shared_sb = work.tile([P, ROUND, U, E], F32)
+            nc.scalar.copy(out=shared_sb[:].rearrange("b i u e -> b i (u e)"), in_=shared_ps[:])
+            shared_prod = work.tile([P, ROUND, SOURCES, U, E], F32)
+            for i in range(ROUND):
+                n = r * ROUND + i
+                nc.gpsimd.tensor_tensor(
+                    out=shared_prod[:, i],
+                    in0=shared_sb[:, i].unsqueeze(1).to_broadcast([P, SOURCES, U, E]),
+                    in1=gates_shared[:, n].unsqueeze(2).to_broadcast([P, SOURCES, U, E]),
+                    op=ALU.mult,
+                )
+            shared_sum = shared_sums[r % 2]
+            nc.vector.tensor_reduce(
+                out=shared_sum[:, :, 0:SLOTS_USED],
+                in_=shared_prod[:].rearrange("b i o u e -> b i (o u) e"),
+                axis=AXIS_X,
+                op=ALU.add,
+            )
+
+            sums_ps = ps_misc.tile([P, ROUND, P], F32, tag="misc")
+            for i in range(ROUND):
+                n = r * ROUND + i
+                own_ps = ps_ra.tile([P, T, E, U], F32)
+                for t in range(T):
+                    nc.tensor.transpose(
+                        out=own_ps[:, t].rearrange("b e u -> b (e u)"),
+                        in_=experts[:, t, i * P : (i + 1) * P],
+                        identity=ident[:],
+                    )
+                own_prod = prod.tile([P, E, 2, T, U], F32)
+                for h in range(2):
+                    nc.vector.tensor_tensor(
+                        out=own_prod[:, :, h, :, :],
+                        in0=own_ps[:].rearrange("b t e u -> b e t u"),
+                        in1=gates_own[:, n, h].unsqueeze(3).to_broadcast([P, E, T, U]),
+                        op=ALU.mult,
+                    )
+                for e in range(E):
+                    nc.tensor.matmul(
+                        out=sums_ps[:, i, :],
+                        lhsT=own_prod[:, e].rearrange("b h t u -> b (h t u)"),
+                        rhs=ident[:],
+                        is_transpose=True,
+                        start=(e == 0),
+                        stop=False,
+                    )
+                nc.tensor.matmul(
+                    out=sums_ps[:, i, :],
+                    lhsT=shared_sum[:, i, :],
+                    rhs=ident[:],
+                    is_transpose=True,
+                    start=False,
+                    stop=True,
+                )
+
+            sums_sb = work.tile([P, ROUND, P], F32)
+            nc.scalar.copy(out=sums_sb[:], in_=sums_ps[:])
+            back_ps = ps_misc.tile([P, ROUND, 2, T, U], F32, tag="misc")
+            for i in range(ROUND):
+                nc.tensor.transpose(
+                    out=back_ps[:, i].rearrange("b h t u -> b (h t u)"),
+                    in_=sums_sb[:, i, :],
+                    identity=ident[:],
+                )
+            first = r % STORE_ROUNDS == 0
+            if first:
+                stage_task = work.tile([P, T, STORE_ROUNDS * ROUND, U], F32)
+                stage_share = work.tile([P, STORE_ROUNDS * ROUND, U], F32)
+            at = (r % STORE_ROUNDS) * ROUND
+            nc.scalar.copy(
+                out=stage_task[:, :, at : at + ROUND, :],
+                in_=back_ps[:, :, 0].rearrange("b i t u -> b t i u"),
+            )
+            share_parts = work.tile([P, ROUND, T, U], F32)
+            nc.scalar.copy(out=share_parts[:], in_=back_ps[:, :, 1])
+            nc.vector.tensor_reduce(
+                out=stage_share[:, at : at + ROUND, :],
+                in_=share_parts[:].rearrange("b i t u -> b i u t"),
+                axis=AXIS_X,
+                op=ALU.add,
+            )
+            if r % STORE_ROUNDS == STORE_ROUNDS - 1:
+                n0 = (r + 1 - STORE_ROUNDS) * ROUND
+                n1 = (r + 1) * ROUND
+                nc.sync.dma_start(out=out_task_rows[:, :, n0:n1, :], in_=stage_task[:])
+                nc.sync.dma_start(out=out_share_rows[:, n0:n1, :], in_=stage_share[:])

@@ -41,21 +41,40 @@ def tile_plelayer_pa_t_kernel(
         keep = ctx.enter_context(tc.tile_pool(name="keep", bufs=1))
         gate_tmp = ctx.enter_context(tc.tile_pool(name="gate_tmp", bufs=2))
         x_pool = ctx.enter_context(tc.tile_pool(name="x_pool", bufs=3))
-        quant = ctx.enter_context(tc.tile_pool(name="quant", bufs=2))
         work = ctx.enter_context(tc.tile_pool(name="work", bufs=2))
-        prod = ctx.enter_context(tc.tile_pool(name="prod", bufs=6))
+        prod = ctx.enter_context(tc.tile_pool(name="prod", bufs=2 * ROUND))
         ps_xt = ctx.enter_context(tc.psum_pool(name="ps_xt", bufs=2))
         ps_y = ctx.enter_context(tc.psum_pool(name="ps_y", bufs=2))
-        ps_ra = ctx.enter_context(tc.psum_pool(name="ps_ra", bufs=2))
+        ps_own = ctx.enter_context(tc.psum_pool(name="ps_own", bufs=2))
         ps_misc = ctx.enter_context(tc.psum_pool(name="ps_misc", bufs=2))
+        ctx.enter_context(tc.manual_schedule())
 
         x_rows = x.rearrange("(p n) k -> p n k", n=ROW_TILES)
         out_task_rows = out_0.rearrange("t (p n) u -> p t n u", n=ROW_TILES)
         out_share_rows = out_1.rearrange("(p n) u -> p n u", n=ROW_TILES)
 
-        ident = keep.tile([P, P], F32)
-        make_identity(nc, ident[:])
-
+        SHARED_ROW = 32
+        bias_rows = keep.tile([P, UE], BF16)
+        nc.scalar.dma_start(out=bias_rows[0:T, :], in_=eb0.rearrange("t u e -> t (u e)"))
+        nc.scalar.dma_start(
+            out=bias_rows[SHARED_ROW : SHARED_ROW + 1, :],
+            in_=ebs0.rearrange("(o u) e -> o (u e)", o=1),
+        )
+        gate_bias_task = keep.tile([P, T, G_TASK], BF16)
+        nc.scalar.dma_start(
+            out=gate_bias_task[:].rearrange("p t k -> p (t k)"),
+            in_=gb0.rearrange("t k -> (t k)").partition_broadcast(P),
+        )
+        gate_bias_share = keep.tile([P, G_SHARE], BF16)
+        nc.scalar.dma_start(out=gate_bias_share[:], in_=gbs.partition_broadcast(P))
+        pre_task = keep.tile([P, T, ROW_TILES, G_TASK], BF16)
+        nc.scalar.dma_start(
+            out=pre_task[:], in_=gate_pre0.rearrange("t (p n) k -> p t n k", n=ROW_TILES)
+        )
+        pre_share = keep.tile([P, ROW_TILES, G_SHARE], BF16)
+        nc.scalar.dma_start(
+            out=pre_share[:], in_=sgate_pre.rearrange("(p n) k -> p n k", n=ROW_TILES)
+        )
         w_raw = keep.tile([P, SOURCES, 2 * PASSES, 2, UE], BF16)
         for t in range(T):
             nc.sync.dma_start(
@@ -67,23 +86,150 @@ def tile_plelayer_pa_t_kernel(
             in_=ews0.rearrange("(a q c) u e -> q a c (u e)", a=2 * PASSES, c=2),
         )
 
+        x_tiles = {}
+
         def load_x(r):
             x_sb = x_pool.tile([P, ROUND, D], BF16)
             nc.sync.dma_start(out=x_sb[:], in_=x_rows[:, r * ROUND : (r + 1) * ROUND, :])
-            return x_sb
+            x_tiles[r] = x_sb
 
-        x_first = load_x(0)
+        X_AHEAD = 3
+        for r in range(X_AHEAD):
+            load_x(r)
+
+        ident = keep.tile([P, P], F32)
+        make_identity(nc, ident[:])
+
+        gates_own = keep.tile([P, ROW_TILES, 2, E, T], F32)
+        gates_shared = keep.tile([P, ROW_TILES, SOURCES, E], F32)
+
+        def gates_logits(job):
+            rows, count = job["rows"], job["count"]
+            task_tile = gate_tmp.tile([P, T, GATE_CHUNK, G_TASK], F32)
+            share_tile = gate_tmp.tile([P, GATE_CHUNK, G_SHARE], F32)
+            job["task"] = task_tile[:, :, 0:count, :]
+            job["share"] = share_tile[:, 0:count, :]
+            nc.gpsimd.tensor_tensor(
+                out=job["task"],
+                in0=pre_task[:, :, rows, :],
+                in1=gate_bias_task[:].unsqueeze(2).to_broadcast([P, T, count, G_TASK]),
+                op=ALU.add,
+            )
+            nc.gpsimd.tensor_tensor(
+                out=job["share"],
+                in0=pre_share[:, rows, :],
+                in1=gate_bias_share[:].unsqueeze(1).to_broadcast([P, count, G_SHARE]),
+                op=ALU.add,
+            )
+
+        def gates_shift(job):
+            count = job["count"]
+            task_top = gate_tmp.tile([P, T, GATE_CHUNK], F32)
+            share_top = gate_tmp.tile([P, GATE_CHUNK], F32)
+            nc.vector.tensor_reduce(
+                out=task_top[:, :, 0:count], in_=job["task"], axis=AXIS_X, op=ALU.max
+            )
+            nc.vector.tensor_reduce(
+                out=share_top[:, 0:count], in_=job["share"], axis=AXIS_X, op=ALU.max
+            )
+            nc.gpsimd.tensor_tensor(
+                out=job["task"],
+                in0=job["task"],
+                in1=task_top[:, :, 0:count].unsqueeze(3).to_broadcast([P, T, count, G_TASK]),
+                op=ALU.subtract,
+            )
+            nc.gpsimd.tensor_tensor(
+                out=job["share"],
+                in0=job["share"],
+                in1=share_top[:, 0:count].unsqueeze(2).to_broadcast([P, count, G_SHARE]),
+                op=ALU.subtract,
+            )
+
+        def gates_exp(job):
+            nc.scalar.activation(out=job["task"], in_=job["task"], func=ACT.Exp)
+            nc.scalar.activation(out=job["share"], in_=job["share"], func=ACT.Exp)
+
+        def gates_scale(job):
+            rows, count = job["rows"], job["count"]
+            task_sum = gate_tmp.tile([P, T, GATE_CHUNK], F32)
+            share_sum = gate_tmp.tile([P, GATE_CHUNK], F32)
+            nc.vector.tensor_reduce(
+                out=task_sum[:, :, 0:count], in_=job["task"], axis=AXIS_X, op=ALU.add
+            )
+            nc.vector.tensor_reduce(
+                out=share_sum[:, 0:count], in_=job["share"], axis=AXIS_X, op=ALU.add
+            )
+            task_inv = gate_tmp.tile([P, T, GATE_CHUNK], F32)
+            share_inv = gate_tmp.tile([P, GATE_CHUNK], F32)
+            nc.vector.reciprocal(out=task_inv[:, :, 0:count], in_=task_sum[:, :, 0:count])
+            nc.vector.reciprocal(out=share_inv[:, 0:count], in_=share_sum[:, 0:count])
+            task_inv_nt = task_inv[:, :, 0:count].rearrange("p t n -> p n t")
+            share_inv_n = share_inv[:, 0:count]
+            nc.gpsimd.tensor_tensor(
+                out=gates_shared[:, rows, 0:T, :],
+                in0=job["task"][:, :, :, E:G_TASK].rearrange("p t n e -> p n t e"),
+                in1=task_inv_nt.unsqueeze(3).to_broadcast([P, count, T, E]),
+                op=ALU.mult,
+            )
+            nc.gpsimd.tensor_tensor(
+                out=gates_shared[:, rows, SHARED, :],
+                in0=job["share"][:, :, T * E : G_SHARE],
+                in1=share_inv_n.unsqueeze(2).to_broadcast([P, count, E]),
+                op=ALU.mult,
+            )
+            nc.gpsimd.tensor_tensor(
+                out=gates_own[:, rows, 0, :, :],
+                in0=job["task"][:, :, :, 0:E].rearrange("p t n e -> p n e t"),
+                in1=task_inv_nt.unsqueeze(2).to_broadcast([P, count, E, T]),
+                op=ALU.mult,
+            )
+            nc.gpsimd.tensor_tensor(
+                out=gates_own[:, rows, 1, :, :],
+                in0=job["share"][:, :, 0 : T * E].rearrange("p n (t e) -> p n e t", t=T),
+                in1=share_inv_n.unsqueeze(2).unsqueeze(3).to_broadcast([P, count, E, T]),
+                op=ALU.mult,
+            )
+
+        gate_stages = [gates_logits, gates_shift, gates_exp, gates_scale]
+
+        def gate_job(first_slot, first_row_tile, count):
+            return {
+                "first_slot": first_slot,
+                "rows": slice(first_row_tile, first_row_tile + count),
+                "count": count,
+            }
+
+        chunk_rounds = GATE_CHUNK // ROUND
+        first_job = gate_job(None, 0, ROUND)
+        gate_jobs = [gate_job(-len(gate_stages), ROUND, GATE_CHUNK - ROUND)]
+        for chunk in range(1, ROW_TILES // GATE_CHUNK):
+            gate_jobs.append(
+                gate_job(chunk * chunk_rounds - len(gate_stages) - 1, chunk * GATE_CHUNK, GATE_CHUNK)
+            )
+
+        shared_sum_a = keep.tile([P, ROUND, P], F32)
+        shared_sum_b = keep.tile([P, ROUND, P], F32)
+        shared_sums = [shared_sum_a, shared_sum_b]
+        bias_square = keep.tile([P, P], F32)
+        nc.vector.memset(bias_square[:], 0.0)
+        for shared_sum in shared_sums:
+            nc.vector.memset(shared_sum[:], 0.0)
+
+        gates_logits(first_job)
+        gates_shift(first_job)
 
         w_grouped = keep.tile([P, PASSES, SOURCES, UE, PACK], BF16, align_bytes=64)
         w_codes = keep.tile([P, PASSES, SOURCES * UE], U32, align_bytes=64)
         w_scales = keep.tile([P, PASSES, SOURCES * UE], U8, align_bytes=64)
+        VECTOR_GROUPS = 3
         for g in range(PASSES):
             for t in range(T):
-                nc.vector.tensor_copy(
+                regroup = nc.vector.tensor_copy if t < VECTOR_GROUPS else nc.scalar.copy
+                regroup(
                     out=w_grouped[:, g, t].rearrange("q (e u) (a c) -> q e u a c", e=E, a=2),
                     in_=w_raw[:, t, 2 * g : 2 * g + 2].rearrange("q a c (u e) -> q e u a c", u=U),
                 )
-            nc.vector.tensor_copy(
+            nc.scalar.copy(
                 out=w_grouped[:, g, SHARED].rearrange("q k (a c) -> q k a c", a=2),
                 in_=w_raw[:, SHARED, 2 * g : 2 * g + 2].rearrange("q a c k -> q k a c"),
             )
@@ -99,15 +245,6 @@ def tile_plelayer_pa_t_kernel(
                 in_=w_grouped[:, g, SHARED].rearrange("q k j -> q (k j)"),
             )
 
-        SHARED_ROW = 32
-        bias_rows = keep.tile([P, UE], BF16)
-        nc.scalar.dma_start(out=bias_rows[0:T, :], in_=eb0.rearrange("t u e -> t (u e)"))
-        nc.scalar.dma_start(
-            out=bias_rows[SHARED_ROW : SHARED_ROW + 1, :],
-            in_=ebs0.rearrange("(o u) e -> o (u e)", o=1),
-        )
-        bias_square = keep.tile([P, P], F32)
-        nc.vector.memset(bias_square[:], 0.0)
         nc.vector.tensor_copy(
             out=bias_square[0:T, :].rearrange("t (e u) -> t e u", e=E),
             in_=bias_rows[0:T, :].rearrange("t (u e) -> t e u", e=E),
@@ -122,238 +259,202 @@ def tile_plelayer_pa_t_kernel(
         nc.vector.tensor_copy(out=bias_cols[:], in_=bias_ps[:])
         bias_col_of = [t for t in range(T)] + [SHARED_ROW]
 
-        gate_bias_task = keep.tile([P, T, G_TASK], BF16)
-        nc.scalar.dma_start(
-            out=gate_bias_task[:].rearrange("p t k -> p (t k)"),
-            in_=gb0.rearrange("t k -> (t k)").partition_broadcast(P),
-        )
-        gate_bias_share = keep.tile([P, G_SHARE], BF16)
-        nc.scalar.dma_start(out=gate_bias_share[:], in_=gbs.partition_broadcast(P))
-        pre_task = keep.tile([P, T, ROW_TILES, G_TASK], BF16)
-        for t in range(T):
-            nc.scalar.dma_start(
-                out=pre_task[:, t], in_=gate_pre0[t].rearrange("(p n) k -> p n k", n=ROW_TILES)
-            )
-        pre_share = keep.tile([P, ROW_TILES, G_SHARE], BF16)
-        nc.scalar.dma_start(
-            out=pre_share[:], in_=sgate_pre.rearrange("(p n) k -> p n k", n=ROW_TILES)
-        )
+        gates_exp(first_job)
+        gates_scale(first_job)
 
-        gates_own = keep.tile([P, ROW_TILES, 2, E, T], F32)
-        gates_shared = keep.tile([P, ROW_TILES, SOURCES, E], F32)
+        x_grouped, x_codes, x_scales = {}, {}, {}
+        experts, shared_prod, own_prod = {}, {}, {}
+        sums_ps, sums_sb, share_parts = {}, {}, {}
+        stage_task, stage_share = {}, {}
 
-        def softmax_in_place(logits, groups_shape, width):
-            full_shape = [P] + groups_shape + [width]
-            last = len(groups_shape) + 1
-            top = gate_tmp.tile([P] + groups_shape, F32, name="top", tag="top%d" % width)
-            nc.vector.tensor_reduce(out=top[:], in_=logits[:], axis=AXIS_X, op=ALU.max)
-            nc.gpsimd.tensor_tensor(
-                out=logits[:],
-                in0=logits[:],
-                in1=top[:].unsqueeze(last).to_broadcast(full_shape),
-                op=ALU.subtract,
-            )
-            nc.scalar.activation(out=logits[:], in_=logits[:], func=ACT.Exp)
-            total = gate_tmp.tile([P] + groups_shape, F32, name="total", tag="total%d" % width)
-            nc.vector.tensor_reduce(out=total[:], in_=logits[:], axis=AXIS_X, op=ALU.add)
-            inverse = gate_tmp.tile([P] + groups_shape, F32, name="inverse", tag="inv%d" % width)
-            nc.vector.reciprocal(out=inverse[:], in_=total[:])
-            return inverse
-
-        def make_gates(chunk):
-            rows = slice(chunk * GATE_CHUNK, (chunk + 1) * GATE_CHUNK)
-            C = GATE_CHUNK
-            task = gate_tmp.tile([P, T, C, G_TASK], F32)
-            nc.gpsimd.tensor_tensor(
-                out=task[:],
-                in0=pre_task[:, :, rows, :],
-                in1=gate_bias_task[:].unsqueeze(2).to_broadcast([P, T, C, G_TASK]),
-                op=ALU.add,
-            )
-            share = gate_tmp.tile([P, C, G_SHARE], F32)
-            nc.gpsimd.tensor_tensor(
-                out=share[:],
-                in0=pre_share[:, rows, :],
-                in1=gate_bias_share[:].unsqueeze(1).to_broadcast([P, C, G_SHARE]),
-                op=ALU.add,
-            )
-            task_inv = softmax_in_place(task, [T, C], G_TASK)
-            share_inv = softmax_in_place(share, [C], G_SHARE)
-            task_inv_nt = task_inv[:].rearrange("p t n -> p n t")
-            nc.gpsimd.tensor_tensor(
-                out=gates_own[:, rows, 0, :, :],
-                in0=task[:, :, :, 0:E].rearrange("p t n e -> p n e t"),
-                in1=task_inv_nt.unsqueeze(2).to_broadcast([P, C, E, T]),
-                op=ALU.mult,
-            )
-            nc.gpsimd.tensor_tensor(
-                out=gates_shared[:, rows, 0:T, :],
-                in0=task[:, :, :, E:G_TASK].rearrange("p t n e -> p n t e"),
-                in1=task_inv_nt.unsqueeze(3).to_broadcast([P, C, T, E]),
-                op=ALU.mult,
-            )
-            nc.gpsimd.tensor_tensor(
-                out=gates_own[:, rows, 1, :, :],
-                in0=share[:, :, 0 : T * E].rearrange("p n (t e) -> p n e t", t=T),
-                in1=share_inv[:].unsqueeze(2).unsqueeze(3).to_broadcast([P, C, E, T]),
-                op=ALU.mult,
-            )
-            nc.gpsimd.tensor_tensor(
-                out=gates_shared[:, rows, SHARED, :],
-                in0=share[:, :, T * E : G_SHARE],
-                in1=share_inv[:].unsqueeze(2).to_broadcast([P, C, E]),
-                op=ALU.mult,
-            )
-
-        shared_sum_a = keep.tile([P, ROUND, P], F32)
-        shared_sum_b = keep.tile([P, ROUND, P], F32)
-        shared_sums = [shared_sum_a, shared_sum_b]
-        for shared_sum in shared_sums:
-            nc.vector.memset(shared_sum[:], 0.0)
-
-        x_next = x_first
-        for r in range(ROUNDS):
-            if r % (GATE_CHUNK // ROUND) == 0:
-                make_gates(r // (GATE_CHUNK // ROUND))
-            x_sb = x_next
-            if r + 1 < ROUNDS:
-                x_next = load_x(r + 1)
-
-            x_words = x_sb[:].bitcast(F32)
-            x_grouped = quant.tile([P, PASSES, ROUND, P, PACK], BF16, align_bytes=64)
-            x_grouped_words = x_grouped[:].bitcast(F32)
-            for i in range(ROUND):
-                xt_ps = ps_xt.tile([P, 2 * PASSES, P], F32)
-                for a in range(2 * PASSES):
-                    nc.tensor.transpose(
-                        out=xt_ps[:, a, :],
-                        in_=x_words[:, i, a * P : (a + 1) * P],
-                        identity=ident[:],
-                    )
-                nc.scalar.copy(
-                    out=x_grouped_words[:, :, i, :, :],
-                    in_=xt_ps[:].rearrange("q (g a) b -> q g b a", g=PASSES),
+        def transpose_x(r, i):
+            if i == 0:
+                x_grouped[r] = work.tile(
+                    [P, PASSES, ROUND, P, PACK], BF16, align_bytes=64, name="x_grouped"
                 )
-            x_codes = quant.tile([P, PASSES, COLS], U32, align_bytes=64)
-            x_scales = quant.tile([P, PASSES, COLS], U8, align_bytes=64)
+            xt_ps = ps_xt.tile([P, 2 * PASSES, P], F32)
+            for a in range(2 * PASSES):
+                nc.tensor.transpose(
+                    out=xt_ps[:, a, :],
+                    in_=x_tiles[r][:].bitcast(F32)[:, i, a * P : (a + 1) * P],
+                    identity=ident[:],
+                )
+            nc.scalar.copy(
+                out=x_grouped[r][:].bitcast(F32)[:, :, i, :, :],
+                in_=xt_ps[:].rearrange("q (g a) b -> q g b a", g=PASSES),
+            )
+
+        def quantize_x(r):
+            x_codes[r] = work.tile([P, PASSES, COLS], U32, align_bytes=64, name="x_codes")
+            x_scales[r] = work.tile([P, PASSES, COLS], U8, align_bytes=64, name="x_scales")
             for g in range(PASSES):
                 nc.vector.quantize_mx(
-                    out=x_codes[:, g, :].bitcast(FP8X4),
-                    scales=x_scales[:, g, :],
-                    in_=x_grouped[:, g].rearrange("q i b j -> q (i b j)"),
+                    out=x_codes[r][:, g, :].bitcast(FP8X4),
+                    scales=x_scales[r][:, g, :],
+                    in_=x_grouped[r][:, g].rearrange("q i b j -> q (i b j)"),
                 )
 
-            experts = work.tile([P, SOURCES, COLS], F32)
-            for s in range(SOURCES):
+        def expert_matmuls(r):
+            experts[r] = work.tile([P, SOURCES, COLS], F32, name="experts")
+            for s in [SHARED] + [t for t in range(T)]:
                 y_ps = ps_y.tile([P, COLS], F32)
                 for g in range(PASSES):
                     nc.tensor.matmul_mx(
                         out=y_ps[:],
                         lhsT=w_codes[:, g, s * UE : (s + 1) * UE].bitcast(FP8X4),
                         lhsT_scale=w_scales[:, g, s * UE : (s + 1) * UE],
-                        rhs=x_codes[:, g, :].bitcast(FP8X4),
-                        rhs_scale=x_scales[:, g, :],
+                        rhs=x_codes[r][:, g, :].bitcast(FP8X4),
+                        rhs_scale=x_scales[r][:, g, :],
                         start=(g == 0),
                         stop=(g == PASSES - 1),
                     )
                 nc.scalar.activation(
-                    out=experts[:, s, :],
+                    out=experts[r][:, s, :],
                     in_=y_ps[:],
                     func=ACT.Relu,
                     bias=bias_cols[:, bias_col_of[s] : bias_col_of[s] + 1],
                     scale=1.0,
                 )
 
+        def shared_products(r):
             shared_ps = ps_misc.tile([P, ROUND, UE], F32, tag="misc")
             for i in range(ROUND):
                 nc.tensor.transpose(
                     out=shared_ps[:, i, :],
-                    in_=experts[:, SHARED, i * P : (i + 1) * P],
+                    in_=experts[r][:, SHARED, i * P : (i + 1) * P],
                     identity=ident[:],
                 )
             shared_sb = work.tile([P, ROUND, U, E], F32)
             nc.scalar.copy(out=shared_sb[:].rearrange("b i u e -> b i (u e)"), in_=shared_ps[:])
-            shared_prod = work.tile([P, ROUND, SOURCES, U, E], F32)
-            for i in range(ROUND):
-                n = r * ROUND + i
-                nc.gpsimd.tensor_tensor(
-                    out=shared_prod[:, i],
-                    in0=shared_sb[:, i].unsqueeze(1).to_broadcast([P, SOURCES, U, E]),
-                    in1=gates_shared[:, n].unsqueeze(2).to_broadcast([P, SOURCES, U, E]),
-                    op=ALU.mult,
-                )
-            shared_sum = shared_sums[r % 2]
+            shared_prod[r] = work.tile([P, ROUND, SOURCES, U, E], F32, name="shared_prod")
+            full = [P, ROUND, SOURCES, U, E]
+            nc.gpsimd.tensor_tensor(
+                out=shared_prod[r][:],
+                in0=shared_sb[:].unsqueeze(2).to_broadcast(full),
+                in1=gates_shared[:, r * ROUND : (r + 1) * ROUND].unsqueeze(3).to_broadcast(full),
+                op=ALU.mult,
+            )
+
+        def shared_reduce(r):
             nc.vector.tensor_reduce(
-                out=shared_sum[:, :, 0:SLOTS_USED],
-                in_=shared_prod[:].rearrange("b i o u e -> b i (o u) e"),
+                out=shared_sums[r % 2][:, :, 0:SLOTS_USED],
+                in_=shared_prod[r][:].rearrange("b i o u e -> b i (o u) e"),
                 axis=AXIS_X,
                 op=ALU.add,
             )
 
-            sums_ps = ps_misc.tile([P, ROUND, P], F32, tag="misc")
-            for i in range(ROUND):
-                n = r * ROUND + i
-                own_ps = ps_ra.tile([P, T, E, U], F32)
-                for t in range(T):
-                    nc.tensor.transpose(
-                        out=own_ps[:, t].rearrange("b e u -> b (e u)"),
-                        in_=experts[:, t, i * P : (i + 1) * P],
-                        identity=ident[:],
-                    )
-                own_prod = prod.tile([P, E, 2, T, U], F32)
-                for h in range(2):
-                    nc.vector.tensor_tensor(
-                        out=own_prod[:, :, h, :, :],
-                        in0=own_ps[:].rearrange("b t e u -> b e t u"),
-                        in1=gates_own[:, n, h].unsqueeze(3).to_broadcast([P, E, T, U]),
-                        op=ALU.mult,
-                    )
-                for e in range(E):
-                    nc.tensor.matmul(
-                        out=sums_ps[:, i, :],
-                        lhsT=own_prod[:, e].rearrange("b h t u -> b (h t u)"),
-                        rhs=ident[:],
-                        is_transpose=True,
-                        start=(e == 0),
-                        stop=False,
-                    )
-                nc.tensor.matmul(
-                    out=sums_ps[:, i, :],
-                    lhsT=shared_sum[:, i, :],
-                    rhs=ident[:],
-                    is_transpose=True,
-                    start=False,
-                    stop=True,
+        def own_products(r, i):
+            own_ps = ps_own.tile([P, T, E, U], F32)
+            for t in range(T):
+                nc.tensor.transpose(
+                    out=own_ps[:, t].rearrange("b e u -> b (e u)"),
+                    in_=experts[r][:, t, i * P : (i + 1) * P],
+                    identity=ident[:],
+                )
+            own_prod[(r, i)] = prod.tile([P, E, 2, T, U], F32, name="own_prod")
+            for h in range(2):
+                nc.vector.tensor_tensor(
+                    out=own_prod[(r, i)][:, :, h, :, :],
+                    in0=own_ps[:].rearrange("b t e u -> b e t u"),
+                    in1=gates_own[:, r * ROUND + i, h].unsqueeze(3).to_broadcast([P, E, T, U]),
+                    op=ALU.mult,
                 )
 
-            sums_sb = work.tile([P, ROUND, P], F32)
-            nc.scalar.copy(out=sums_sb[:], in_=sums_ps[:])
+        def sum_over_experts(r, i):
+            if i == 0:
+                sums_ps[r] = ps_misc.tile([P, ROUND, P], F32, tag="misc", name="sums_ps")
+            for e in range(E):
+                nc.tensor.matmul(
+                    out=sums_ps[r][:, i, :],
+                    lhsT=own_prod[(r, i)][:, e].rearrange("b h t u -> b (h t u)"),
+                    rhs=ident[:],
+                    is_transpose=True,
+                    start=(e == 0),
+                    stop=False,
+                )
+            nc.tensor.matmul(
+                out=sums_ps[r][:, i, :],
+                lhsT=shared_sums[r % 2][:, i, :],
+                rhs=ident[:],
+                is_transpose=True,
+                start=False,
+                stop=True,
+            )
+
+        def sums_out(r):
+            sums_sb[r] = work.tile([P, ROUND, P], F32, name="sums_sb")
+            nc.scalar.copy(out=sums_sb[r][:], in_=sums_ps[r][:])
+
+        def transpose_back(r):
             back_ps = ps_misc.tile([P, ROUND, 2, T, U], F32, tag="misc")
             for i in range(ROUND):
                 nc.tensor.transpose(
                     out=back_ps[:, i].rearrange("b h t u -> b (h t u)"),
-                    in_=sums_sb[:, i, :],
+                    in_=sums_sb[r][:, i, :],
                     identity=ident[:],
                 )
-            first = r % STORE_ROUNDS == 0
-            if first:
-                stage_task = work.tile([P, T, STORE_ROUNDS * ROUND, U], F32)
-                stage_share = work.tile([P, STORE_ROUNDS * ROUND, U], F32)
+            batch = r // STORE_ROUNDS
+            if r % STORE_ROUNDS == 0:
+                stage_task[batch] = work.tile(
+                    [P, T, STORE_ROUNDS * ROUND, U], F32, name="stage_task"
+                )
+                stage_share[batch] = work.tile(
+                    [P, STORE_ROUNDS * ROUND, U], F32, name="stage_share"
+                )
             at = (r % STORE_ROUNDS) * ROUND
             nc.scalar.copy(
-                out=stage_task[:, :, at : at + ROUND, :],
+                out=stage_task[batch][:, :, at : at + ROUND, :],
                 in_=back_ps[:, :, 0].rearrange("b i t u -> b t i u"),
             )
-            share_parts = work.tile([P, ROUND, T, U], F32)
-            nc.scalar.copy(out=share_parts[:], in_=back_ps[:, :, 1])
+            share_parts[r] = work.tile([P, ROUND, T, U], F32, name="share_parts")
+            nc.scalar.copy(out=share_parts[r][:], in_=back_ps[:, :, 1])
+
+        def finish(r):
+            batch = r // STORE_ROUNDS
+            at = (r % STORE_ROUNDS) * ROUND
             nc.vector.tensor_reduce(
-                out=stage_share[:, at : at + ROUND, :],
-                in_=share_parts[:].rearrange("b i t u -> b i u t"),
+                out=stage_share[batch][:, at : at + ROUND, :],
+                in_=share_parts[r][:].rearrange("b i t u -> b i u t"),
                 axis=AXIS_X,
                 op=ALU.add,
             )
             if r % STORE_ROUNDS == STORE_ROUNDS - 1:
-                n0 = (r + 1 - STORE_ROUNDS) * ROUND
-                n1 = (r + 1) * ROUND
-                nc.sync.dma_start(out=out_task_rows[:, :, n0:n1, :], in_=stage_task[:])
-                nc.sync.dma_start(out=out_share_rows[:, n0:n1, :], in_=stage_share[:])
+                n0 = batch * STORE_ROUNDS * ROUND
+                n1 = n0 + STORE_ROUNDS * ROUND
+                nc.sync.dma_start(out=out_task_rows[:, :, n0:n1, :], in_=stage_task[batch][:])
+                nc.sync.dma_start(out=out_share_rows[:, n0:n1, :], in_=stage_share[batch][:])
+
+        def live(r):
+            return 0 <= r < ROUNDS
+
+        for s in range(-len(gate_stages), ROUNDS + 2):
+            if live(s):
+                own_products(s, 0)
+                own_products(s, 1)
+            if live(s + 1):
+                expert_matmuls(s + 1)
+            if live(s - 2):
+                transpose_back(s - 2)
+            if live(s + 1):
+                shared_products(s + 1)
+            if live(s + 2):
+                quantize_x(s + 2)
+            if live(s):
+                shared_reduce(s)
+                own_products(s, 2)
+                own_products(s, 3)
+            for i in range(ROUND):
+                if live(s + 3):
+                    transpose_x(s + 3, i)
+                if live(s - 1):
+                    sum_over_experts(s - 1, i)
+            if live(s - 1):
+                sums_out(s - 1)
+            for job in gate_jobs:
+                stage = s - job["first_slot"]
+                if 0 <= stage < len(gate_stages):
+                    gate_stages[stage](job)
+            if live(s - 2):
+                finish(s - 2)
+            if live(s + 3) and live(s + 3 + X_AHEAD):
+                load_x(s + 3 + X_AHEAD)

@@ -68,13 +68,11 @@ def tile_plelayer_pa_t_kernel(
         gate_bias_share = keep.tile([P, G_SHARE], BF16)
         nc.scalar.dma_start(out=gate_bias_share[:], in_=gbs.partition_broadcast(P))
         pre_task = keep.tile([P, T, ROW_TILES, G_TASK], BF16)
-        nc.scalar.dma_start(
-            out=pre_task[:], in_=gate_pre0.rearrange("t (p n) k -> p t n k", n=ROW_TILES)
-        )
         pre_share = keep.tile([P, ROW_TILES, G_SHARE], BF16)
-        nc.scalar.dma_start(
-            out=pre_share[:], in_=sgate_pre.rearrange("(p n) k -> p n k", n=ROW_TILES)
-        )
+        pre_task_rows = gate_pre0.rearrange("t (p n) k -> p t n k", n=ROW_TILES)
+        pre_share_rows = sgate_pre.rearrange("(p n) k -> p n k", n=ROW_TILES)
+        nc.scalar.dma_start(out=pre_task[:, :, 0:ROUND, :], in_=pre_task_rows[:, :, 0:ROUND, :])
+        nc.scalar.dma_start(out=pre_share[:, 0:ROUND, :], in_=pre_share_rows[:, 0:ROUND, :])
         w_raw = keep.tile([P, SOURCES, 2 * PASSES, 2, UE], BF16)
         for t in range(T):
             nc.sync.dma_start(
@@ -94,7 +92,14 @@ def tile_plelayer_pa_t_kernel(
             x_tiles[r] = x_sb
 
         X_AHEAD = 3
-        for r in range(X_AHEAD):
+        load_x(0)
+        nc.sync.dma_start(
+            out=pre_task[:, :, ROUND:ROW_TILES, :], in_=pre_task_rows[:, :, ROUND:ROW_TILES, :]
+        )
+        nc.sync.dma_start(
+            out=pre_share[:, ROUND:ROW_TILES, :], in_=pre_share_rows[:, ROUND:ROW_TILES, :]
+        )
+        for r in range(1, X_AHEAD):
             load_x(r)
 
         ident = keep.tile([P, P], F32)
@@ -215,6 +220,17 @@ def tile_plelayer_pa_t_kernel(
         for shared_sum in shared_sums:
             nc.vector.memset(shared_sum[:], 0.0)
 
+        nc.vector.tensor_copy(
+            out=bias_square[0:T, :].rearrange("t (e u) -> t e u", e=E),
+            in_=bias_rows[0:T, :].rearrange("t (u e) -> t e u", e=E),
+        )
+        nc.vector.tensor_copy(
+            out=bias_square[SHARED_ROW : SHARED_ROW + 1, :],
+            in_=bias_rows[SHARED_ROW : SHARED_ROW + 1, :],
+        )
+        bias_ps = ps_misc.tile([P, P], F32, tag="misc")
+        nc.tensor.transpose(out=bias_ps[:], in_=bias_square[:], identity=ident[:])
+
         gates_logits(first_job)
         gates_shift(first_job)
 
@@ -245,16 +261,6 @@ def tile_plelayer_pa_t_kernel(
                 in_=w_grouped[:, g, SHARED].rearrange("q k j -> q (k j)"),
             )
 
-        nc.vector.tensor_copy(
-            out=bias_square[0:T, :].rearrange("t (e u) -> t e u", e=E),
-            in_=bias_rows[0:T, :].rearrange("t (u e) -> t e u", e=E),
-        )
-        nc.vector.tensor_copy(
-            out=bias_square[SHARED_ROW : SHARED_ROW + 1, :],
-            in_=bias_rows[SHARED_ROW : SHARED_ROW + 1, :],
-        )
-        bias_ps = ps_misc.tile([P, P], F32, tag="misc")
-        nc.tensor.transpose(out=bias_ps[:], in_=bias_square[:], identity=ident[:])
         bias_cols = keep.tile([P, P], F32)
         nc.vector.tensor_copy(out=bias_cols[:], in_=bias_ps[:])
         bias_col_of = [t for t in range(T)] + [SHARED_ROW]
@@ -294,27 +300,28 @@ def tile_plelayer_pa_t_kernel(
                     in_=x_grouped[r][:, g].rearrange("q i b j -> q (i b j)"),
                 )
 
-        def expert_matmuls(r):
-            experts[r] = work.tile([P, SOURCES, COLS], F32, name="experts")
-            for s in [SHARED] + [t for t in range(T)]:
-                y_ps = ps_y.tile([P, COLS], F32)
-                for g in range(PASSES):
-                    nc.tensor.matmul_mx(
-                        out=y_ps[:],
-                        lhsT=w_codes[:, g, s * UE : (s + 1) * UE].bitcast(FP8X4),
-                        lhsT_scale=w_scales[:, g, s * UE : (s + 1) * UE],
-                        rhs=x_codes[r][:, g, :].bitcast(FP8X4),
-                        rhs_scale=x_scales[r][:, g, :],
-                        start=(g == 0),
-                        stop=(g == PASSES - 1),
-                    )
-                nc.scalar.activation(
-                    out=experts[r][:, s, :],
-                    in_=y_ps[:],
-                    func=ACT.Relu,
-                    bias=bias_cols[:, bias_col_of[s] : bias_col_of[s] + 1],
-                    scale=1.0,
+        def expert_group(r, group):
+            if group == SHARED:
+                experts[r] = work.tile([P, SOURCES, COLS], F32, name="experts")
+            columns = slice(group * UE, (group + 1) * UE)
+            y_ps = ps_y.tile([P, COLS], F32)
+            for g in range(PASSES):
+                nc.tensor.matmul_mx(
+                    out=y_ps[:],
+                    lhsT=w_codes[:, g, columns].bitcast(FP8X4),
+                    lhsT_scale=w_scales[:, g, columns],
+                    rhs=x_codes[r][:, g, :].bitcast(FP8X4),
+                    rhs_scale=x_scales[r][:, g, :],
+                    start=(g == 0),
+                    stop=(g == PASSES - 1),
                 )
+            nc.scalar.activation(
+                out=experts[r][:, group, :],
+                in_=y_ps[:],
+                func=ACT.Relu,
+                bias=bias_cols[:, bias_col_of[group] : bias_col_of[group] + 1],
+                scale=1.0,
+            )
 
         def shared_products(r):
             shared_ps = ps_misc.tile([P, ROUND, UE], F32, tag="misc")
@@ -424,37 +431,30 @@ def tile_plelayer_pa_t_kernel(
                 nc.sync.dma_start(out=out_task_rows[:, :, n0:n1, :], in_=stage_task[batch][:])
                 nc.sync.dma_start(out=out_share_rows[:, n0:n1, :], in_=stage_share[batch][:])
 
-        def live(r):
-            return 0 <= r < ROUNDS
+        def step(make, r, *which):
+            if 0 <= r < ROUNDS:
+                make(r, *which)
 
         for s in range(-len(gate_stages), ROUNDS + 2):
-            if live(s):
-                own_products(s, 0)
-                own_products(s, 1)
-            if live(s + 1):
-                expert_matmuls(s + 1)
-            if live(s - 2):
-                transpose_back(s - 2)
-            if live(s + 1):
-                shared_products(s + 1)
-            if live(s + 2):
-                quantize_x(s + 2)
-            if live(s):
-                shared_reduce(s)
-                own_products(s, 2)
-                own_products(s, 3)
+            step(own_products, s, 0)
+            step(own_products, s, 1)
+            step(expert_group, s + 1, SHARED)
+            step(transpose_back, s - 2)
+            step(quantize_x, s + 2)
+            step(shared_reduce, s)
             for i in range(ROUND):
-                if live(s + 3):
-                    transpose_x(s + 3, i)
-                if live(s - 1):
-                    sum_over_experts(s - 1, i)
-            if live(s - 1):
-                sums_out(s - 1)
+                step(transpose_x, s + 3, i)
+                step(expert_group, s + 1, i)
+                if i == 0:
+                    step(shared_products, s + 1)
+                if i + 1 in (2, 3):
+                    step(own_products, s, i + 1)
+                step(sum_over_experts, s - 1, i)
+            step(sums_out, s - 1)
             for job in gate_jobs:
                 stage = s - job["first_slot"]
                 if 0 <= stage < len(gate_stages):
                     gate_stages[stage](job)
-            if live(s - 2):
-                finish(s - 2)
-            if live(s + 3) and live(s + 3 + X_AHEAD):
-                load_x(s + 3 + X_AHEAD)
+            step(finish, s - 2)
+            if s + 3 >= 0:
+                step(load_x, s + 3 + X_AHEAD)

@@ -105,15 +105,33 @@ def tile_plelayer_pa_t_kernel(
         ident = keep.tile([P, P], F32)
         make_identity(nc, ident[:])
 
-        gates_own = keep.tile([P, ROW_TILES, 2, E, T], F32)
+        gates_own = keep.tile([P, ROW_TILES, E, 2, T], F32)
         gates_shared = keep.tile([P, ROW_TILES, SOURCES, E], F32)
+
+        def gate_job(first_row_tile, count):
+            task_tile = gate_tmp.tile([P, T, GATE_CHUNK, G_TASK], F32)
+            share_tile = gate_tmp.tile([P, GATE_CHUNK, G_SHARE], F32)
+            task_top = gate_tmp.tile([P, T, GATE_CHUNK], F32)
+            share_top = gate_tmp.tile([P, GATE_CHUNK], F32)
+            task_sum = gate_tmp.tile([P, T, GATE_CHUNK], F32)
+            share_sum = gate_tmp.tile([P, GATE_CHUNK], F32)
+            task_inv = gate_tmp.tile([P, T, GATE_CHUNK], F32)
+            share_inv = gate_tmp.tile([P, GATE_CHUNK], F32)
+            return {
+                "rows": slice(first_row_tile, first_row_tile + count),
+                "count": count,
+                "task": task_tile[:, :, 0:count, :],
+                "share": share_tile[:, 0:count, :],
+                "task_top": task_top[:, :, 0:count],
+                "share_top": share_top[:, 0:count],
+                "task_sum": task_sum[:, :, 0:count],
+                "share_sum": share_sum[:, 0:count],
+                "task_inv": task_inv[:, :, 0:count],
+                "share_inv": share_inv[:, 0:count],
+            }
 
         def gates_logits(job):
             rows, count = job["rows"], job["count"]
-            task_tile = gate_tmp.tile([P, T, GATE_CHUNK, G_TASK], F32)
-            share_tile = gate_tmp.tile([P, GATE_CHUNK, G_SHARE], F32)
-            job["task"] = task_tile[:, :, 0:count, :]
-            job["share"] = share_tile[:, 0:count, :]
             nc.gpsimd.tensor_tensor(
                 out=job["task"],
                 in0=pre_task[:, :, rows, :],
@@ -127,26 +145,22 @@ def tile_plelayer_pa_t_kernel(
                 op=ALU.add,
             )
 
-        def gates_shift(job):
+        def gates_top(job):
+            nc.vector.tensor_reduce(out=job["task_top"], in_=job["task"], axis=AXIS_X, op=ALU.max)
+            nc.vector.tensor_reduce(out=job["share_top"], in_=job["share"], axis=AXIS_X, op=ALU.max)
+
+        def gates_subtract(job):
             count = job["count"]
-            task_top = gate_tmp.tile([P, T, GATE_CHUNK], F32)
-            share_top = gate_tmp.tile([P, GATE_CHUNK], F32)
-            nc.vector.tensor_reduce(
-                out=task_top[:, :, 0:count], in_=job["task"], axis=AXIS_X, op=ALU.max
-            )
-            nc.vector.tensor_reduce(
-                out=share_top[:, 0:count], in_=job["share"], axis=AXIS_X, op=ALU.max
-            )
             nc.gpsimd.tensor_tensor(
                 out=job["task"],
                 in0=job["task"],
-                in1=task_top[:, :, 0:count].unsqueeze(3).to_broadcast([P, T, count, G_TASK]),
+                in1=job["task_top"].unsqueeze(3).to_broadcast([P, T, count, G_TASK]),
                 op=ALU.subtract,
             )
             nc.gpsimd.tensor_tensor(
                 out=job["share"],
                 in0=job["share"],
-                in1=share_top[:, 0:count].unsqueeze(2).to_broadcast([P, count, G_SHARE]),
+                in1=job["share_top"].unsqueeze(2).to_broadcast([P, count, G_SHARE]),
                 op=ALU.subtract,
             )
 
@@ -154,22 +168,15 @@ def tile_plelayer_pa_t_kernel(
             nc.scalar.activation(out=job["task"], in_=job["task"], func=ACT.Exp)
             nc.scalar.activation(out=job["share"], in_=job["share"], func=ACT.Exp)
 
-        def gates_scale(job):
+        def gates_inverse(job):
+            nc.vector.tensor_reduce(out=job["task_sum"], in_=job["task"], axis=AXIS_X, op=ALU.add)
+            nc.vector.tensor_reduce(out=job["share_sum"], in_=job["share"], axis=AXIS_X, op=ALU.add)
+            nc.vector.reciprocal(out=job["task_inv"], in_=job["task_sum"])
+            nc.vector.reciprocal(out=job["share_inv"], in_=job["share_sum"])
+
+        def gates_write(job):
             rows, count = job["rows"], job["count"]
-            task_sum = gate_tmp.tile([P, T, GATE_CHUNK], F32)
-            share_sum = gate_tmp.tile([P, GATE_CHUNK], F32)
-            nc.vector.tensor_reduce(
-                out=task_sum[:, :, 0:count], in_=job["task"], axis=AXIS_X, op=ALU.add
-            )
-            nc.vector.tensor_reduce(
-                out=share_sum[:, 0:count], in_=job["share"], axis=AXIS_X, op=ALU.add
-            )
-            task_inv = gate_tmp.tile([P, T, GATE_CHUNK], F32)
-            share_inv = gate_tmp.tile([P, GATE_CHUNK], F32)
-            nc.vector.reciprocal(out=task_inv[:, :, 0:count], in_=task_sum[:, :, 0:count])
-            nc.vector.reciprocal(out=share_inv[:, 0:count], in_=share_sum[:, 0:count])
-            task_inv_nt = task_inv[:, :, 0:count].rearrange("p t n -> p n t")
-            share_inv_n = share_inv[:, 0:count]
+            task_inv_nt = job["task_inv"].rearrange("p t n -> p n t")
             nc.gpsimd.tensor_tensor(
                 out=gates_shared[:, rows, 0:T, :],
                 in0=job["task"][:, :, :, E:G_TASK].rearrange("p t n e -> p n t e"),
@@ -179,38 +186,28 @@ def tile_plelayer_pa_t_kernel(
             nc.gpsimd.tensor_tensor(
                 out=gates_shared[:, rows, SHARED, :],
                 in0=job["share"][:, :, T * E : G_SHARE],
-                in1=share_inv_n.unsqueeze(2).to_broadcast([P, count, E]),
+                in1=job["share_inv"].unsqueeze(2).to_broadcast([P, count, E]),
                 op=ALU.mult,
             )
             nc.gpsimd.tensor_tensor(
-                out=gates_own[:, rows, 0, :, :],
+                out=gates_own[:, rows, :, 0, :],
                 in0=job["task"][:, :, :, 0:E].rearrange("p t n e -> p n e t"),
                 in1=task_inv_nt.unsqueeze(2).to_broadcast([P, count, E, T]),
                 op=ALU.mult,
             )
             nc.gpsimd.tensor_tensor(
-                out=gates_own[:, rows, 1, :, :],
+                out=gates_own[:, rows, :, 1, :],
                 in0=job["share"][:, :, 0 : T * E].rearrange("p n (t e) -> p n e t", t=T),
-                in1=share_inv_n.unsqueeze(2).unsqueeze(3).to_broadcast([P, count, E, T]),
+                in1=job["share_inv"].unsqueeze(2).unsqueeze(3).to_broadcast([P, count, E, T]),
                 op=ALU.mult,
             )
 
-        gate_stages = [gates_logits, gates_shift, gates_exp, gates_scale]
-
-        def gate_job(first_slot, first_row_tile, count):
-            return {
-                "first_slot": first_slot,
-                "rows": slice(first_row_tile, first_row_tile + count),
-                "count": count,
-            }
-
-        chunk_rounds = GATE_CHUNK // ROUND
-        first_job = gate_job(None, 0, ROUND)
-        gate_jobs = [gate_job(-len(gate_stages), ROUND, GATE_CHUNK - ROUND)]
+        GATE_LEAD = 3
+        gate_job_rows = {1 - GATE_LEAD: (ROUND, GATE_CHUNK - ROUND)}
         for chunk in range(1, ROW_TILES // GATE_CHUNK):
-            gate_jobs.append(
-                gate_job(chunk * chunk_rounds - len(gate_stages) - 1, chunk * GATE_CHUNK, GATE_CHUNK)
-            )
+            gate_job_rows[chunk * GATE_CHUNK // ROUND - GATE_LEAD] = (chunk * GATE_CHUNK, GATE_CHUNK)
+        gate_jobs = {}
+        first_job = gate_job(0, ROUND)
 
         shared_sum_a = keep.tile([P, ROUND, P], F32)
         shared_sum_b = keep.tile([P, ROUND, P], F32)
@@ -232,7 +229,8 @@ def tile_plelayer_pa_t_kernel(
         nc.tensor.transpose(out=bias_ps[:], in_=bias_square[:], identity=ident[:])
 
         gates_logits(first_job)
-        gates_shift(first_job)
+        gates_top(first_job)
+        gates_subtract(first_job)
 
         w_grouped = keep.tile([P, PASSES, SOURCES, UE, PACK], BF16, align_bytes=64)
         w_codes = keep.tile([P, PASSES, SOURCES * UE], U32, align_bytes=64)
@@ -266,7 +264,8 @@ def tile_plelayer_pa_t_kernel(
         bias_col_of = [t for t in range(T)] + [SHARED_ROW]
 
         gates_exp(first_job)
-        gates_scale(first_job)
+        gates_inverse(first_job)
+        gates_write(first_job)
 
         x_grouped, x_codes, x_scales = {}, {}, {}
         experts, shared_prod, own_prod = {}, {}, {}
@@ -351,21 +350,21 @@ def tile_plelayer_pa_t_kernel(
             )
 
         def own_products(r, i):
-            own_ps = ps_own.tile([P, T, E, U], F32)
+            own_ps = ps_own.tile([P, E, T, U], F32)
             for t in range(T):
                 nc.tensor.transpose(
-                    out=own_ps[:, t].rearrange("b e u -> b (e u)"),
+                    out=own_ps[:, :, t, :],
                     in_=experts[r][:, t, i * P : (i + 1) * P],
                     identity=ident[:],
                 )
             own_prod[(r, i)] = prod.tile([P, E, 2, T, U], F32, name="own_prod")
-            for h in range(2):
-                nc.vector.tensor_tensor(
-                    out=own_prod[(r, i)][:, :, h, :, :],
-                    in0=own_ps[:].rearrange("b t e u -> b e t u"),
-                    in1=gates_own[:, r * ROUND + i, h].unsqueeze(3).to_broadcast([P, E, T, U]),
-                    op=ALU.mult,
-                )
+            full = [P, E, 2, T, U]
+            nc.vector.tensor_tensor(
+                out=own_prod[(r, i)][:],
+                in0=own_ps[:].unsqueeze(2).to_broadcast(full),
+                in1=gates_own[:, r * ROUND + i].unsqueeze(4).to_broadcast(full),
+                op=ALU.mult,
+            )
 
         def sum_over_experts(r, i):
             if i == 0:
@@ -435,7 +434,14 @@ def tile_plelayer_pa_t_kernel(
             if 0 <= r < ROUNDS:
                 make(r, *which)
 
-        for s in range(-len(gate_stages), ROUNDS + 2):
+        for s in range(-GATE_LEAD, ROUNDS + 2):
+            if s in gate_job_rows:
+                gate_jobs[s] = gate_job(*gate_job_rows[s])
+                gates_logits(gate_jobs[s])
+            if s - 1 in gate_jobs:
+                gates_subtract(gate_jobs[s - 1])
+            if s - 2 in gate_jobs:
+                gates_write(gate_jobs[s - 2])
             step(own_products, s, 0)
             step(own_products, s, 1)
             step(expert_group, s + 1, SHARED)
@@ -447,14 +453,16 @@ def tile_plelayer_pa_t_kernel(
                 step(expert_group, s + 1, i)
                 if i == 0:
                     step(shared_products, s + 1)
+                if i == 1 and s - 1 in gate_jobs:
+                    gates_exp(gate_jobs[s - 1])
                 if i + 1 in (2, 3):
                     step(own_products, s, i + 1)
                 step(sum_over_experts, s - 1, i)
             step(sums_out, s - 1)
-            for job in gate_jobs:
-                stage = s - job["first_slot"]
-                if 0 <= stage < len(gate_stages):
-                    gate_stages[stage](job)
+            if s in gate_jobs:
+                gates_top(gate_jobs[s])
+            if s - 1 in gate_jobs:
+                gates_inverse(gate_jobs[s - 1])
             step(finish, s - 2)
             if s + 3 >= 0:
                 step(load_x, s + 3 + X_AHEAD)

@@ -14,23 +14,23 @@ AXIS_X = mybir.AxisListType.X
 
 P = 128
 T, B, D, U, E = 4, 8192, 1024, 16, 8
-SOURCES = T + 1
+GROUPS = T + 1
 SHARED = T
 UE = U * E
 G_TASK = 2 * E
-G_SHARE = SOURCES * E
+G_SHARE = GROUPS * E
 PACK = 4
-K_PASS = P * PACK
-PASSES = D // K_PASS
+PASSES = D // (P * PACK)
+HALVES = 2 * PASSES
 ROW_TILES = B // P
 ROUND = 4
 ROUNDS = ROW_TILES // ROUND
 COLS = ROUND * P
 GATE_CHUNK = 16
-STORE_ROUNDS = 4
-SLOTS_USED = SOURCES * U
+STORE_ROUNDS = 2
+SHARED_ROW = 32
 
-FLOPS = 2 * B * D * SOURCES * UE
+FLOPS = 2 * B * D * GROUPS * UE
 
 
 def tile_plelayer_pa_t_kernel(
@@ -50,10 +50,11 @@ def tile_plelayer_pa_t_kernel(
         ctx.enter_context(tc.manual_schedule())
 
         x_rows = x.rearrange("(p n) k -> p n k", n=ROW_TILES)
+        pre_task_rows = gate_pre0.rearrange("t (p n) k -> p t n k", n=ROW_TILES)
+        pre_share_rows = sgate_pre.rearrange("(p n) k -> p n k", n=ROW_TILES)
         out_task_rows = out_0.rearrange("t (p n) u -> p t n u", n=ROW_TILES)
         out_share_rows = out_1.rearrange("(p n) u -> p n u", n=ROW_TILES)
 
-        SHARED_ROW = 32
         bias_rows = keep.tile([P, UE], BF16)
         nc.scalar.dma_start(out=bias_rows[0:T, :], in_=eb0.rearrange("t u e -> t (u e)"))
         nc.scalar.dma_start(
@@ -69,27 +70,22 @@ def tile_plelayer_pa_t_kernel(
         nc.scalar.dma_start(out=gate_bias_share[:], in_=gbs.partition_broadcast(P))
         pre_task = keep.tile([P, T, ROW_TILES, G_TASK], BF16)
         pre_share = keep.tile([P, ROW_TILES, G_SHARE], BF16)
-        pre_task_rows = gate_pre0.rearrange("t (p n) k -> p t n k", n=ROW_TILES)
-        pre_share_rows = sgate_pre.rearrange("(p n) k -> p n k", n=ROW_TILES)
         nc.scalar.dma_start(out=pre_task[:, :, 0:ROUND, :], in_=pre_task_rows[:, :, 0:ROUND, :])
         nc.scalar.dma_start(out=pre_share[:, 0:ROUND, :], in_=pre_share_rows[:, 0:ROUND, :])
-        w_raw = keep.tile([P, SOURCES, 2 * PASSES, 2, UE], BF16)
+        w_raw = keep.tile([P, GROUPS, HALVES, 2, UE], BF16)
         for t in range(T):
             nc.sync.dma_start(
-                out=w_raw[:, t],
-                in_=ew0[t].rearrange("(a q c) u e -> q a c (u e)", a=2 * PASSES, c=2),
+                out=w_raw[:, t], in_=ew0[t].rearrange("(a q c) u e -> q a c (u e)", a=HALVES, c=2)
             )
         nc.sync.dma_start(
-            out=w_raw[:, SHARED],
-            in_=ews0.rearrange("(a q c) u e -> q a c (u e)", a=2 * PASSES, c=2),
+            out=w_raw[:, SHARED], in_=ews0.rearrange("(a q c) u e -> q a c (u e)", a=HALVES, c=2)
         )
 
         x_tiles = {}
 
         def load_x(r):
-            x_sb = x_pool.tile([P, ROUND, D], BF16)
-            nc.sync.dma_start(out=x_sb[:], in_=x_rows[:, r * ROUND : (r + 1) * ROUND, :])
-            x_tiles[r] = x_sb
+            x_tiles[r] = x_pool.tile([P, ROUND, D], BF16, name="x_sb")
+            nc.sync.dma_start(out=x_tiles[r][:], in_=x_rows[:, r * ROUND : (r + 1) * ROUND, :])
 
         X_AHEAD = 3
         load_x(0)
@@ -105,8 +101,59 @@ def tile_plelayer_pa_t_kernel(
         ident = keep.tile([P, P], F32)
         make_identity(nc, ident[:])
 
+        bias_square = keep.tile([P, P], F32)
+        nc.vector.memset(bias_square[:], 0.0)
+        nc.vector.tensor_copy(
+            out=bias_square[0:T, :].rearrange("t (e u) -> t e u", e=E),
+            in_=bias_rows[0:T, :].rearrange("t (u e) -> t e u", e=E),
+        )
+        nc.vector.tensor_copy(
+            out=bias_square[SHARED_ROW : SHARED_ROW + 1, :],
+            in_=bias_rows[SHARED_ROW : SHARED_ROW + 1, :],
+        )
+        bias_ps = ps_misc.tile([P, P], F32, tag="misc")
+        nc.tensor.transpose(out=bias_ps[:], in_=bias_square[:], identity=ident[:])
+        bias_cols = keep.tile([P, P], F32)
+        nc.vector.tensor_copy(out=bias_cols[:], in_=bias_ps[:])
+        bias_col_of = [t for t in range(T)] + [SHARED_ROW]
+
+        shared_sum_even = keep.tile([P, ROUND, P], F32)
+        shared_sum_odd = keep.tile([P, ROUND, P], F32)
+        shared_sums = [shared_sum_even, shared_sum_odd]
+        for shared_sum in shared_sums:
+            nc.vector.memset(shared_sum[:], 0.0)
+
+        w_codes = keep.tile([P, PASSES, GROUPS * UE], U32, align_bytes=64)
+        w_scales = keep.tile([P, PASSES, GROUPS * UE], U8, align_bytes=64)
+
+        def prepare_weights():
+            w_grouped = keep.tile([P, PASSES, GROUPS, UE, PACK], BF16, align_bytes=64)
+            vector_groups = 3
+            for g in range(PASSES):
+                for t in range(T):
+                    regroup = nc.vector.tensor_copy if t < vector_groups else nc.scalar.copy
+                    regroup(
+                        out=w_grouped[:, g, t].rearrange("q (e u) (a c) -> q e u a c", e=E, a=2),
+                        in_=w_raw[:, t, 2 * g : 2 * g + 2].rearrange("q a c (u e) -> q e u a c", u=U),
+                    )
+                nc.scalar.copy(
+                    out=w_grouped[:, g, SHARED].rearrange("q k (a c) -> q k a c", a=2),
+                    in_=w_raw[:, SHARED, 2 * g : 2 * g + 2].rearrange("q a c k -> q k a c"),
+                )
+            for g in range(PASSES):
+                nc.vector.quantize_mx(
+                    out=w_codes[:, g, 0 : T * UE].bitcast(FP8X4),
+                    scales=w_scales[:, g, 0 : T * UE],
+                    in_=w_grouped[:, g, 0:T].rearrange("q s k j -> q (s k j)"),
+                )
+                nc.vector.quantize_mx(
+                    out=w_codes[:, g, T * UE : GROUPS * UE].bitcast(FP8X4),
+                    scales=w_scales[:, g, T * UE : GROUPS * UE],
+                    in_=w_grouped[:, g, SHARED].rearrange("q k j -> q (k j)"),
+                )
+
         gates_own = keep.tile([P, ROW_TILES, E, 2, T], F32)
-        gates_shared = keep.tile([P, ROW_TILES, SOURCES, E], F32)
+        gates_shared = keep.tile([P, ROW_TILES, GROUPS, E], F32)
 
         def gate_job(first_row_tile, count):
             task_tile = gate_tmp.tile([P, T, GATE_CHUNK, G_TASK], F32)
@@ -202,70 +249,11 @@ def tile_plelayer_pa_t_kernel(
                 op=ALU.mult,
             )
 
-        GATE_LEAD = 3
-        gate_job_rows = {1 - GATE_LEAD: (ROUND, GATE_CHUNK - ROUND)}
-        for chunk in range(1, ROW_TILES // GATE_CHUNK):
-            gate_job_rows[chunk * GATE_CHUNK // ROUND - GATE_LEAD] = (chunk * GATE_CHUNK, GATE_CHUNK)
+        GATE_LEAD = 4
+        gate_job_rows = {-GATE_LEAD: (0, ROUND), 1 - GATE_LEAD: (ROUND, GATE_CHUNK - ROUND)}
+        for first_row_tile in range(GATE_CHUNK, ROW_TILES, GATE_CHUNK):
+            gate_job_rows[first_row_tile // ROUND - GATE_LEAD] = (first_row_tile, GATE_CHUNK)
         gate_jobs = {}
-        first_job = gate_job(0, ROUND)
-
-        shared_sum_a = keep.tile([P, ROUND, P], F32)
-        shared_sum_b = keep.tile([P, ROUND, P], F32)
-        shared_sums = [shared_sum_a, shared_sum_b]
-        bias_square = keep.tile([P, P], F32)
-        nc.vector.memset(bias_square[:], 0.0)
-        for shared_sum in shared_sums:
-            nc.vector.memset(shared_sum[:], 0.0)
-
-        nc.vector.tensor_copy(
-            out=bias_square[0:T, :].rearrange("t (e u) -> t e u", e=E),
-            in_=bias_rows[0:T, :].rearrange("t (u e) -> t e u", e=E),
-        )
-        nc.vector.tensor_copy(
-            out=bias_square[SHARED_ROW : SHARED_ROW + 1, :],
-            in_=bias_rows[SHARED_ROW : SHARED_ROW + 1, :],
-        )
-        bias_ps = ps_misc.tile([P, P], F32, tag="misc")
-        nc.tensor.transpose(out=bias_ps[:], in_=bias_square[:], identity=ident[:])
-
-        gates_logits(first_job)
-        gates_top(first_job)
-        gates_subtract(first_job)
-
-        w_grouped = keep.tile([P, PASSES, SOURCES, UE, PACK], BF16, align_bytes=64)
-        w_codes = keep.tile([P, PASSES, SOURCES * UE], U32, align_bytes=64)
-        w_scales = keep.tile([P, PASSES, SOURCES * UE], U8, align_bytes=64)
-        VECTOR_GROUPS = 3
-        for g in range(PASSES):
-            for t in range(T):
-                regroup = nc.vector.tensor_copy if t < VECTOR_GROUPS else nc.scalar.copy
-                regroup(
-                    out=w_grouped[:, g, t].rearrange("q (e u) (a c) -> q e u a c", e=E, a=2),
-                    in_=w_raw[:, t, 2 * g : 2 * g + 2].rearrange("q a c (u e) -> q e u a c", u=U),
-                )
-            nc.scalar.copy(
-                out=w_grouped[:, g, SHARED].rearrange("q k (a c) -> q k a c", a=2),
-                in_=w_raw[:, SHARED, 2 * g : 2 * g + 2].rearrange("q a c k -> q k a c"),
-            )
-        for g in range(PASSES):
-            nc.vector.quantize_mx(
-                out=w_codes[:, g, 0 : T * UE].bitcast(FP8X4),
-                scales=w_scales[:, g, 0 : T * UE],
-                in_=w_grouped[:, g, 0:T].rearrange("q s k j -> q (s k j)"),
-            )
-            nc.vector.quantize_mx(
-                out=w_codes[:, g, T * UE : SOURCES * UE].bitcast(FP8X4),
-                scales=w_scales[:, g, T * UE : SOURCES * UE],
-                in_=w_grouped[:, g, SHARED].rearrange("q k j -> q (k j)"),
-            )
-
-        bias_cols = keep.tile([P, P], F32)
-        nc.vector.tensor_copy(out=bias_cols[:], in_=bias_ps[:])
-        bias_col_of = [t for t in range(T)] + [SHARED_ROW]
-
-        gates_exp(first_job)
-        gates_inverse(first_job)
-        gates_write(first_job)
 
         x_grouped, x_codes, x_scales = {}, {}, {}
         experts, shared_prod, own_prod = {}, {}, {}
@@ -277,8 +265,8 @@ def tile_plelayer_pa_t_kernel(
                 x_grouped[r] = work.tile(
                     [P, PASSES, ROUND, P, PACK], BF16, align_bytes=64, name="x_grouped"
                 )
-            xt_ps = ps_xt.tile([P, 2 * PASSES, P], F32)
-            for a in range(2 * PASSES):
+            xt_ps = ps_xt.tile([P, HALVES, P], F32)
+            for a in range(HALVES):
                 nc.tensor.transpose(
                     out=xt_ps[:, a, :],
                     in_=x_tiles[r][:].bitcast(F32)[:, i, a * P : (a + 1) * P],
@@ -301,7 +289,7 @@ def tile_plelayer_pa_t_kernel(
 
         def expert_group(r, group):
             if group == SHARED:
-                experts[r] = work.tile([P, SOURCES, COLS], F32, name="experts")
+                experts[r] = work.tile([P, GROUPS, COLS], F32, name="experts")
             columns = slice(group * UE, (group + 1) * UE)
             y_ps = ps_y.tile([P, COLS], F32)
             for g in range(PASSES):
@@ -332,8 +320,8 @@ def tile_plelayer_pa_t_kernel(
                 )
             shared_sb = work.tile([P, ROUND, U, E], F32)
             nc.scalar.copy(out=shared_sb[:].rearrange("b i u e -> b i (u e)"), in_=shared_ps[:])
-            shared_prod[r] = work.tile([P, ROUND, SOURCES, U, E], F32, name="shared_prod")
-            full = [P, ROUND, SOURCES, U, E]
+            shared_prod[r] = work.tile([P, ROUND, GROUPS, U, E], F32, name="shared_prod")
+            full = [P, ROUND, GROUPS, U, E]
             nc.gpsimd.tensor_tensor(
                 out=shared_prod[r][:],
                 in0=shared_sb[:].unsqueeze(2).to_broadcast(full),
@@ -343,7 +331,7 @@ def tile_plelayer_pa_t_kernel(
 
         def shared_reduce(r):
             nc.vector.tensor_reduce(
-                out=shared_sums[r % 2][:, :, 0:SLOTS_USED],
+                out=shared_sums[r % 2][:, :, 0 : GROUPS * U],
                 in_=shared_prod[r][:].rearrange("b i o u e -> b i (o u) e"),
                 axis=AXIS_X,
                 op=ALU.add,
@@ -434,14 +422,16 @@ def tile_plelayer_pa_t_kernel(
             if 0 <= r < ROUNDS:
                 make(r, *which)
 
+        def gate_step(make, first_slot):
+            if first_slot in gate_jobs:
+                make(gate_jobs[first_slot])
+
         for s in range(-GATE_LEAD, ROUNDS + 2):
             if s in gate_job_rows:
                 gate_jobs[s] = gate_job(*gate_job_rows[s])
-                gates_logits(gate_jobs[s])
-            if s - 1 in gate_jobs:
-                gates_subtract(gate_jobs[s - 1])
-            if s - 2 in gate_jobs:
-                gates_write(gate_jobs[s - 2])
+            gate_step(gates_write, s - 3)
+            gate_step(gates_subtract, s - 1)
+            gate_step(gates_logits, s)
             step(own_products, s, 0)
             step(own_products, s, 1)
             step(expert_group, s + 1, SHARED)
@@ -453,16 +443,15 @@ def tile_plelayer_pa_t_kernel(
                 step(expert_group, s + 1, i)
                 if i == 0:
                     step(shared_products, s + 1)
-                if i == 1 and s - 1 in gate_jobs:
-                    gates_exp(gate_jobs[s - 1])
-                if i + 1 in (2, 3):
+                elif i + 1 < ROUND:
                     step(own_products, s, i + 1)
                 step(sum_over_experts, s - 1, i)
             step(sums_out, s - 1)
-            if s in gate_jobs:
-                gates_top(gate_jobs[s])
-            if s - 1 in gate_jobs:
-                gates_inverse(gate_jobs[s - 1])
+            gate_step(gates_exp, s - 1)
+            gate_step(gates_top, s)
+            gate_step(gates_inverse, s - 2)
             step(finish, s - 2)
+            if s == -GATE_LEAD:
+                prepare_weights()
             if s + 3 >= 0:
                 step(load_x, s + 3 + X_AHEAD)

from contextlib import ExitStack

import concourse.mybir as mybir
from concourse.masks import make_identity

F32 = mybir.dt.float32
BF16 = mybir.dt.bfloat16
U32 = mybir.dt.uint32
U8 = mybir.dt.uint8
FP8X4 = mybir.dt.float8_e4m3fn_x4
ALU = mybir.AluOpType
ACT = mybir.ActivationFunctionType
AXIS_X = mybir.AxisListType.X

P = 128
T, B, D, U, E = 4, 8192, 1024, 16, 8
GROUPS = T + 1
SHARED = T
UE = U * E
G_TASK = 2 * E
G_SHARE = GROUPS * E
PACK = 4
PASSES = D // (P * PACK)
HALVES = 2 * PASSES
ROW_TILES = B // P
ROUND = 4
ROUNDS = ROW_TILES // ROUND
COLS = ROUND * P
GATE_CHUNK = 16
STORE_ROUNDS = 2
SHARED_ROW = 32

FLOPS = 2 * B * D * GROUPS * UE


def tile_plelayer_pa_t_kernel(
    tc, x, ews0, ebs0, ew0, eb0, gate_pre0, gb0, sgate_pre, gbs, out_0, out_1
):
    nc = tc.nc
    with ExitStack() as ctx:
        keep = ctx.enter_context(tc.tile_pool(name="keep", bufs=1))
        gate_tmp = ctx.enter_context(tc.tile_pool(name="gate_tmp", bufs=2))
        x_pool = ctx.enter_context(tc.tile_pool(name="x_pool", bufs=3))
        work = ctx.enter_context(tc.tile_pool(name="work", bufs=2))
        prod = ctx.enter_context(tc.tile_pool(name="prod", bufs=2 * ROUND))
        ps_xt = ctx.enter_context(tc.psum_pool(name="ps_xt", bufs=2))
        ps_y = ctx.enter_context(tc.psum_pool(name="ps_y", bufs=2))
        ps_own = ctx.enter_context(tc.psum_pool(name="ps_own", bufs=2))
        ps_misc = ctx.enter_context(tc.psum_pool(name="ps_misc", bufs=2))
        ctx.enter_context(tc.manual_schedule())

        x_rows = x.rearrange("(p n) k -> p n k", n=ROW_TILES)
        pre_task_rows = gate_pre0.rearrange("t (p n) k -> p t n k", n=ROW_TILES)
        pre_share_rows = sgate_pre.rearrange("(p n) k -> p n k", n=ROW_TILES)
        out_task_rows = out_0.rearrange("t (p n) u -> p t n u", n=ROW_TILES)
        out_share_rows = out_1.rearrange("(p n) u -> p n u", n=ROW_TILES)

        bias_rows = keep.tile([P, UE], BF16)
        nc.scalar.dma_start(out=bias_rows[0:T, :], in_=eb0.rearrange("t u e -> t (u e)"))
        nc.scalar.dma_start(
            out=bias_rows[SHARED_ROW : SHARED_ROW + 1, :],
            in_=ebs0.rearrange("(o u) e -> o (u e)", o=1),
        )
        gate_bias_task = keep.tile([P, T, G_TASK], BF16)
        nc.scalar.dma_start(
            out=gate_bias_task[:].rearrange("p t k -> p (t k)"),
            in_=gb0.rearrange("t k -> (t k)").partition_broadcast(P),
        )
        gate_bias_share = keep.tile([P, G_SHARE], BF16)
        nc.scalar.dma_start(out=gate_bias_share[:], in_=gbs.partition_broadcast(P))
        pre_task = keep.tile([P, T, ROW_TILES, G_TASK], BF16)
        pre_share = keep.tile([P, ROW_TILES, G_SHARE], BF16)
        nc.scalar.dma_start(out=pre_task[:, :, 0:ROUND, :], in_=pre_task_rows[:, :, 0:ROUND, :])
        nc.scalar.dma_start(out=pre_share[:, 0:ROUND, :], in_=pre_share_rows[:, 0:ROUND, :])
        w_raw = keep.tile([P, GROUPS, HALVES, 2, UE], BF16)
        for t in range(T):
            nc.sync.dma_start(
                out=w_raw[:, t], in_=ew0[t].rearrange("(a q c) u e -> q a c (u e)", a=HALVES, c=2)
            )
        nc.sync.dma_start(
            out=w_raw[:, SHARED], in_=ews0.rearrange("(a q c) u e -> q a c (u e)", a=HALVES, c=2)
        )

        x_tiles = {}

        def load_x(r):
            x_tiles[r] = x_pool.tile([P, ROUND, D], BF16, name="x_sb")
            nc.sync.dma_start(out=x_tiles[r][:], in_=x_rows[:, r * ROUND : (r + 1) * ROUND, :])

        X_AHEAD = 3
        load_x(0)
        nc.sync.dma_start(
            out=pre_task[:, :, ROUND:ROW_TILES, :], in_=pre_task_rows[:, :, ROUND:ROW_TILES, :]
        )
        nc.sync.dma_start(
            out=pre_share[:, ROUND:ROW_TILES, :], in_=pre_share_rows[:, ROUND:ROW_TILES, :]
        )
        for r in range(1, X_AHEAD):
            load_x(r)

        ident = keep.tile([P, P], F32)
        make_identity(nc, ident[:])

        bias_square = keep.tile([P, P], F32)
        nc.vector.memset(bias_square[:], 0.0)
        nc.vector.tensor_copy(
            out=bias_square[0:T, :].rearrange("t (e u) -> t e u", e=E),
            in_=bias_rows[0:T, :].rearrange("t (u e) -> t e u", e=E),
        )
        nc.vector.tensor_copy(
            out=bias_square[SHARED_ROW : SHARED_ROW + 1, :],
            in_=bias_rows[SHARED_ROW : SHARED_ROW + 1, :],
        )
        bias_ps = ps_misc.tile([P, P], F32, tag="misc")
        nc.tensor.transpose(out=bias_ps[:], in_=bias_square[:], identity=ident[:])
        bias_cols = keep.tile([P, P], F32)
        nc.vector.tensor_copy(out=bias_cols[:], in_=bias_ps[:])
        bias_col_of = [t for t in range(T)] + [SHARED_ROW]

        shared_sum_even = keep.tile([P, ROUND, P], F32)
        shared_sum_odd = keep.tile([P, ROUND, P], F32)
        shared_sums = [shared_sum_even, shared_sum_odd]
        for shared_sum in shared_sums:
            nc.vector.memset(shared_sum[:], 0.0)

        w_codes = keep.tile([P, PASSES, GROUPS * UE], U32, align_bytes=64)
        w_scales = keep.tile([P, PASSES, GROUPS * UE], U8, align_bytes=64)

        def prepare_weights():
            w_grouped = keep.tile([P, PASSES, GROUPS, UE, PACK], BF16, align_bytes=64)
            vector_groups = 3
            for g in range(PASSES):
                for t in range(T):
                    regroup = nc.vector.tensor_copy if t < vector_groups else nc.scalar.copy
                    regroup(
                        out=w_grouped[:, g, t].rearrange("q (e u) (a c) -> q e u a c", e=E, a=2),
                        in_=w_raw[:, t, 2 * g : 2 * g + 2].rearrange("q a c (u e) -> q e u a c", u=U),
                    )
                nc.scalar.copy(
                    out=w_grouped[:, g, SHARED].rearrange("q k (a c) -> q k a c", a=2),
                    in_=w_raw[:, SHARED, 2 * g : 2 * g + 2].rearrange("q a c k -> q k a c"),
                )
            for g in range(PASSES):
                nc.vector.quantize_mx(
                    out=w_codes[:, g, 0 : T * UE].bitcast(FP8X4),
                    scales=w_scales[:, g, 0 : T * UE],
                    in_=w_grouped[:, g, 0:T].rearrange("q s k j -> q (s k j)"),
                )
                nc.vector.quantize_mx(
                    out=w_codes[:, g, T * UE : GROUPS * UE].bitcast(FP8X4),
                    scales=w_scales[:, g, T * UE : GROUPS * UE],
                    in_=w_grouped[:, g, SHARED].rearrange("q k j -> q (k j)"),
                )

        gates_own = keep.tile([P, ROW_TILES, E, 2, T], F32)
        gates_shared = keep.tile([P, ROW_TILES, GROUPS, E], F32)

        def gate_job(first_row_tile, count):
            task_tile = gate_tmp.tile([P, T, GATE_CHUNK, G_TASK], F32)
            share_tile = gate_tmp.tile([P, GATE_CHUNK, G_SHARE], F32)
            task_top = gate_tmp.tile([P, T, GATE_CHUNK], F32)
            share_top = gate_tmp.tile([P, GATE_CHUNK], F32)
            task_sum = gate_tmp.tile([P, T, GATE_CHUNK], F32)
            share_sum = gate_tmp.tile([P, GATE_CHUNK], F32)
            task_inv = gate_tmp.tile([P, T, GATE_CHUNK], F32)
            share_inv = gate_tmp.tile([P, GATE_CHUNK], F32)
            return {
                "rows": slice(first_row_tile, first_row_tile + count),
                "count": count,
                "task": task_tile[:, :, 0:count, :],
                "share": share_tile[:, 0:count, :],
                "task_top": task_top[:, :, 0:count],
                "share_top": share_top[:, 0:count],
                "task_sum": task_sum[:, :, 0:count],
                "share_sum": share_sum[:, 0:count],
                "task_inv": task_inv[:, :, 0:count],
                "share_inv": share_inv[:, 0:count],
            }

        def gates_logits(job):
            rows, count = job["rows"], job["count"]
            nc.gpsimd.tensor_tensor(
                out=job["task"],
                in0=pre_task[:, :, rows, :],
                in1=gate_bias_task[:].unsqueeze(2).to_broadcast([P, T, count, G_TASK]),
                op=ALU.add,
            )
            nc.gpsimd.tensor_tensor(
                out=job["share"],
                in0=pre_share[:, rows, :],
                in1=gate_bias_share[:].unsqueeze(1).to_broadcast([P, count, G_SHARE]),
                op=ALU.add,
            )

        def gates_top(job):
            nc.vector.tensor_reduce(out=job["task_top"], in_=job["task"], axis=AXIS_X, op=ALU.max)
            nc.vector.tensor_reduce(out=job["share_top"], in_=job["share"], axis=AXIS_X, op=ALU.max)

        def gates_subtract(job):
            count = job["count"]
            nc.gpsimd.tensor_tensor(
                out=job["task"],
                in0=job["task"],
                in1=job["task_top"].unsqueeze(3).to_broadcast([P, T, count, G_TASK]),
                op=ALU.subtract,
            )
            nc.gpsimd.tensor_tensor(
                out=job["share"],
                in0=job["share"],
                in1=job["share_top"].unsqueeze(2).to_broadcast([P, count, G_SHARE]),
                op=ALU.subtract,
            )

        def gates_exp(job):
            nc.scalar.activation(out=job["task"], in_=job["task"], func=ACT.Exp)
            nc.scalar.activation(out=job["share"], in_=job["share"], func=ACT.Exp)

        def gates_inverse(job):
            nc.vector.tensor_reduce(out=job["task_sum"], in_=job["task"], axis=AXIS_X, op=ALU.add)
            nc.vector.tensor_reduce(out=job["share_sum"], in_=job["share"], axis=AXIS_X, op=ALU.add)
            nc.vector.reciprocal(out=job["task_inv"], in_=job["task_sum"])
            nc.vector.reciprocal(out=job["share_inv"], in_=job["share_sum"])

        def gates_write(job):
            rows, count = job["rows"], job["count"]
            task_inv_nt = job["task_inv"].rearrange("p t n -> p n t")
            nc.gpsimd.tensor_tensor(
                out=gates_shared[:, rows, 0:T, :],
                in0=job["task"][:, :, :, E:G_TASK].rearrange("p t n e -> p n t e"),
                in1=task_inv_nt.unsqueeze(3).to_broadcast([P, count, T, E]),
                op=ALU.mult,
            )
            nc.gpsimd.tensor_tensor(
                out=gates_shared[:, rows, SHARED, :],
                in0=job["share"][:, :, T * E : G_SHARE],
                in1=job["share_inv"].unsqueeze(2).to_broadcast([P, count, E]),
                op=ALU.mult,
            )
            nc.gpsimd.tensor_tensor(
                out=gates_own[:, rows, :, 0, :],
                in0=job["task"][:, :, :, 0:E].rearrange("p t n e -> p n e t"),
                in1=task_inv_nt.unsqueeze(2).to_broadcast([P, count, E, T]),
                op=ALU.mult,
            )
            nc.gpsimd.tensor_tensor(
                out=gates_own[:, rows, :, 1, :],
                in0=job["share"][:, :, 0 : T * E].rearrange("p n (t e) -> p n e t", t=T),
                in1=job["share_inv"].unsqueeze(2).unsqueeze(3).to_broadcast([P, count, E, T]),
                op=ALU.mult,
            )

        GATE_LEAD = 4
        gate_job_rows = {-GATE_LEAD: (0, ROUND), 1 - GATE_LEAD: (ROUND, GATE_CHUNK - ROUND)}
        for first_row_tile in range(GATE_CHUNK, ROW_TILES, GATE_CHUNK):
            gate_job_rows[first_row_tile // ROUND - GATE_LEAD] = (first_row_tile, GATE_CHUNK)
        gate_jobs = {}

        x_grouped, x_codes, x_scales = {}, {}, {}
        experts, shared_prod, own_prod = {}, {}, {}
        sums_ps, sums_sb, share_parts = {}, {}, {}
        stage_task, stage_share = {}, {}

        def transpose_x(r, i):
            if i == 0:
                x_grouped[r] = work.tile(
                    [P, PASSES, ROUND, P, PACK], BF16, align_bytes=64, name="x_grouped"
                )
            xt_ps = ps_xt.tile([P, HALVES, P], F32)
            for a in range(HALVES):
                nc.tensor.transpose(
                    out=xt_ps[:, a, :],
                    in_=x_tiles[r][:].bitcast(F32)[:, i, a * P : (a + 1) * P],
                    identity=ident[:],
                )
            nc.scalar.copy(
                out=x_grouped[r][:].bitcast(F32)[:, :, i, :, :],
                in_=xt_ps[:].rearrange("q (g a) b -> q g b a", g=PASSES),
            )

        def quantize_x(r):
            x_codes[r] = work.tile([P, PASSES, COLS], U32, align_bytes=64, name="x_codes")
            x_scales[r] = work.tile([P, PASSES, COLS], U8, align_bytes=64, name="x_scales")
            for g in range(PASSES):
                nc.vector.quantize_mx(
                    out=x_codes[r][:, g, :].bitcast(FP8X4),
                    scales=x_scales[r][:, g, :],
                    in_=x_grouped[r][:, g].rearrange("q i b j -> q (i b j)"),
                )

        def expert_group(r, group):
            if group == SHARED:
                experts[r] = work.tile([P, GROUPS, COLS], F32, name="experts")
            columns = slice(group * UE, (group + 1) * UE)
            y_ps = ps_y.tile([P, COLS], F32)
            for g in range(PASSES):
                nc.tensor.matmul_mx(
                    out=y_ps[:],
                    lhsT=w_codes[:, g, columns].bitcast(FP8X4),
                    lhsT_scale=w_scales[:, g, columns],
                    rhs=x_codes[r][:, g, :].bitcast(FP8X4),
                    rhs_scale=x_scales[r][:, g, :],
                    start=(g == 0),
                    stop=(g == PASSES - 1),
                )
            nc.scalar.activation(
                out=experts[r][:, group, :],
                in_=y_ps[:],
                func=ACT.Relu,
                bias=bias_cols[:, bias_col_of[group] : bias_col_of[group] + 1],
                scale=1.0,
            )

        def shared_products(r):
            shared_ps = ps_misc.tile([P, ROUND, UE], F32, tag="misc")
            for i in range(ROUND):
                nc.tensor.transpose(
                    out=shared_ps[:, i, :],
                    in_=experts[r][:, SHARED, i * P : (i + 1) * P],
                    identity=ident[:],
                )
            shared_sb = work.tile([P, ROUND, U, E], F32)
            nc.scalar.copy(out=shared_sb[:].rearrange("b i u e -> b i (u e)"), in_=shared_ps[:])
            shared_prod[r] = work.tile([P, ROUND, GROUPS, U, E], F32, name="shared_prod")
            full = [P, ROUND, GROUPS, U, E]
            nc.gpsimd.tensor_tensor(
                out=shared_prod[r][:],
                in0=shared_sb[:].unsqueeze(2).to_broadcast(full),
                in1=gates_shared[:, r * ROUND : (r + 1) * ROUND].unsqueeze(3).to_broadcast(full),
                op=ALU.mult,
            )

        def shared_reduce(r):
            nc.vector.tensor_reduce(
                out=shared_sums[r % 2][:, :, 0 : GROUPS * U],
                in_=shared_prod[r][:].rearrange("b i o u e -> b i (o u) e"),
                axis=AXIS_X,
                op=ALU.add,
            )

        def own_products(r, i):
            own_ps = ps_own.tile([P, E, T, U], F32)
            for t in range(T):
                nc.tensor.transpose(
                    out=own_ps[:, :, t, :],
                    in_=experts[r][:, t, i * P : (i + 1) * P],
                    identity=ident[:],
                )
            own_prod[(r, i)] = prod.tile([P, E, 2, T, U], F32, name="own_prod")
            full = [P, E, 2, T, U]
            nc.vector.tensor_tensor(
                out=own_prod[(r, i)][:],
                in0=own_ps[:].unsqueeze(2).to_broadcast(full),
                in1=gates_own[:, r * ROUND + i].unsqueeze(4).to_broadcast(full),
                op=ALU.mult,
            )

        def sum_over_experts(r, i):
            if i == 0:
                sums_ps[r] = ps_misc.tile([P, ROUND, P], F32, tag="misc", name="sums_ps")
            for e in range(E):
                nc.tensor.matmul(
                    out=sums_ps[r][:, i, :],
                    lhsT=own_prod[(r, i)][:, e].rearrange("b h t u -> b (h t u)"),
                    rhs=ident[:],
                    is_transpose=True,
                    start=(e == 0),
                    stop=False,
                )
            nc.tensor.matmul(
                out=sums_ps[r][:, i, :],
                lhsT=shared_sums[r % 2][:, i, :],
                rhs=ident[:],
                is_transpose=True,
                start=False,
                stop=True,
            )

        def sums_out(r):
            sums_sb[r] = work.tile([P, ROUND, P], F32, name="sums_sb")
            nc.scalar.copy(out=sums_sb[r][:], in_=sums_ps[r][:])

        def transpose_back(r):
            back_ps = ps_misc.tile([P, ROUND, 2, T, U], F32, tag="misc")
            for i in range(ROUND):
                nc.tensor.transpose(
                    out=back_ps[:, i].rearrange("b h t u -> b (h t u)"),
                    in_=sums_sb[r][:, i, :],
                    identity=ident[:],
                )
            batch = r // STORE_ROUNDS
            if r % STORE_ROUNDS == 0:
                stage_task[batch] = work.tile(
                    [P, T, STORE_ROUNDS * ROUND, U], F32, name="stage_task"
                )
                stage_share[batch] = work.tile(
                    [P, STORE_ROUNDS * ROUND, U], F32, name="stage_share"
                )
            at = (r % STORE_ROUNDS) * ROUND
            nc.scalar.copy(
                out=stage_task[batch][:, :, at : at + ROUND, :],
                in_=back_ps[:, :, 0].rearrange("b i t u -> b t i u"),
            )
            share_parts[r] = work.tile([P, ROUND, T, U], F32, name="share_parts")
            nc.scalar.copy(out=share_parts[r][:], in_=back_ps[:, :, 1])

        def finish(r):
            batch = r // STORE_ROUNDS
            at = (r % STORE_ROUNDS) * ROUND
            nc.vector.tensor_reduce(
                out=stage_share[batch][:, at : at + ROUND, :],
                in_=share_parts[r][:].rearrange("b i t u -> b i u t"),
                axis=AXIS_X,
                op=ALU.add,
            )
            if r % STORE_ROUNDS == STORE_ROUNDS - 1:
                n0 = batch * STORE_ROUNDS * ROUND
                n1 = n0 + STORE_ROUNDS * ROUND
                nc.sync.dma_start(out=out_task_rows[:, :, n0:n1, :], in_=stage_task[batch][:])
                nc.sync.dma_start(out=out_share_rows[:, n0:n1, :], in_=stage_share[batch][:])

        def step(make, r, *which):
            if 0 <= r < ROUNDS:
                make(r, *which)

        def gate_step(make, first_slot):
            if first_slot in gate_jobs:
                make(gate_jobs[first_slot])

        for s in range(-GATE_LEAD, ROUNDS + 2):
            if s in gate_job_rows:
                gate_jobs[s] = gate_job(*gate_job_rows[s])
            gate_step(gates_write, s - 3)
            gate_step(gates_subtract, s - 1)
            gate_step(gates_logits, s)
            step(own_products, s, 0)
            step(own_products, s, 1)
            step(expert_group, s + 1, SHARED)
            step(transpose_back, s - 2)
            step(quantize_x, s + 2)
            step(shared_reduce, s)
            for i in range(ROUND):
                step(transpose_x, s + 3, i)
                step(expert_group, s + 1, i)
                if i == 0:
                    step(shared_products, s + 1)
                elif i + 1 < ROUND:
                    step(own_products, s, i + 1)
                step(sum_over_experts, s - 1, i)
            step(sums_out, s - 1)
            gate_step(gates_exp, s - 1)
            gate_step(gates_top, s)
            gate_step(gates_inverse, s - 2)
            step(finish, s - 2)
            if s == -GATE_LEAD:
                prepare_weights()
            if s + 3 >= 0:
                step(load_x, s + 3 + X_AHEAD)
